import numpy as np
import ml_dtypes


def mxq(x, axis, fmt="e4m3"):
    dtype, down = {"e4m3": (ml_dtypes.float8_e4m3fn, 7), "e5m2": (ml_dtypes.float8_e5m2, 14)}[fmt]
    v = np.moveaxis(np.asarray(x, np.float32).astype(ml_dtypes.bfloat16).astype(np.float64), axis, -1)
    blocks = v.reshape(v.shape[:-1] + (-1, 32))
    amax = np.abs(blocks).max(-1, keepdims=True)
    byte = np.maximum(np.where(amax > 0, np.frexp(amax)[1] - 1 + 127, 0) - down, 1)
    scale = np.exp2(byte - 127.0)
    codes = (blocks / scale).astype(np.float32).astype(dtype).astype(np.float64)
    return np.moveaxis((codes * scale).reshape(v.shape), -1, axis)


WIDE = False


def mx_kscale(k):
    if not WIDE:
        return np.ones(k)
    levels = np.array([10, -10, 5, -5, 0])
    a = np.random.permutation(np.resize(levels, k // 512 * 4)).reshape(k // 512, 4)
    idx = np.arange(k)
    return np.exp2(a[idx // 512, idx % 128 // 32])


BF16 = ml_dtypes.bfloat16


def bf(x):
    return np.asarray(x, np.float32).astype(BF16)


def f64(x):
    return np.asarray(x).astype(np.float64)


N, T, B, C, H = 512, 3, 2, 512, 512
N3 = T * N
O = H + H


def sigmoid(v):
    return 1.0 / (1.0 + np.exp(-v))


def setup_inputs():
    s = np.array(mx_kscale(N3))
    s[N:N + N] = 1.0
    shape = (N3, B, H)
    h1 = np.random.standard_normal(shape) * sigmoid(np.random.standard_normal(shape))
    return {"h1": bf(h1 * s[:, None, None]),
            "A_mid": bf(np.random.standard_normal((N, N3)) / np.sqrt(N3) / s[None, :]),
            "W1": bf(np.random.standard_normal((O, H)) * 1.5 / np.sqrt(H)),
            "b1": bf(np.random.standard_normal(O) * 0.3)}


def reference(h1, A_mid, W1, b1):
    h1 = f64(h1)
    h = h1.transpose(1, 2, 0)
    g = mxq(h, 2, "e4m3") @ mxq(f64(A_mid), 1, "e4m3").T
    y = (mxq(f64(W1), 1, "e4m3") @ mxq(g, 1, "e4m3")) + f64(b1)[None, :, None]
    h2 = y[:, :H] * sigmoid(y[:, H:])
    return np.maximum(h1[N:N + N], h2.transpose(2, 0, 1))

@@ -1,0 +1,224 @@
+from contextlib import ExitStack
+
+import concourse.mybir as mybir
+from concourse.masks import make_identity
+
+F32 = mybir.dt.float32
+BF16 = mybir.dt.bfloat16
+U32 = mybir.dt.uint32
+U8 = mybir.dt.uint8
+FP8X4 = mybir.dt.float8_e4m3fn_x4
+ACT = mybir.ActivationFunctionType
+ALU = mybir.AluOpType
+
+P = 128
+PACK = 4
+N_TARGET = 512
+N_SOURCE = 1536
+B = 2
+C = 512
+O = 2 * C
+W_PASSES = N_SOURCE // (P * PACK)
+HALF = 256
+J_TILES = C // P
+
+FLOPS = 2 * B * C * N_TARGET * N_SOURCE + 2 * B * O * C * N_TARGET
+
+
+def tile_stsgcm_pb_kernel(tc, h1, A_mid, W1, b1, out):
+    nc = tc.nc
+    with ExitStack() as stack:
+        keep = stack.enter_context(tc.tile_pool(name="keep", bufs=1))
+        work = stack.enter_context(tc.tile_pool(name="work", bufs=4))
+        psum_t = stack.enter_context(tc.psum_pool(name="psum_t", bufs=2))
+        psum_g = stack.enter_context(tc.psum_pool(name="psum_g", bufs=2))
+        psum_y = stack.enter_context(tc.psum_pool(name="psum_y", bufs=4))
+
+        ident_f32 = keep.tile([P, P], F32, name="ident_f32")
+        nc.vector.memset(ident_f32[:], 0.0)
+        make_identity(nc, ident_f32[:], nomemset=True)
+        ident_bf16 = keep.tile([P, P], BF16, name="ident_bf16")
+        nc.vector.tensor_copy(out=ident_bf16[:], in_=ident_f32[:])
+        warm_in = keep.tile([P, 1], F32, name="warm_in")
+        warm_out = keep.tile([P, 1], F32, name="warm_out")
+        nc.vector.memset(warm_in[:], 0.0)
+        nc.scalar.activation(out=warm_out[:], in_=warm_in[:], func=ACT.Sigmoid)
+        bias_rows = keep.tile([P, P], BF16, name="bias_rows")
+        nc.vector.memset(bias_rows[:], 0.0)
+        nc.scalar.dma_start(out=bias_rows[0 : O // P, :], in_=b1.rearrange("(t p) -> t p", p=P))
+
+        a_raw = [keep.tile([P, 2, N_SOURCE], BF16, name="a_raw%d" % u) for u in range(2)]
+        h_raw = [[keep.tile([P, PACK, C], BF16, name="h_raw%d_%d" % (b, s)) for s in range(W_PASSES)] for b in range(B)]
+        w_raw = [keep.tile([P, 2, C], BF16, name="w_raw%d" % jt) for jt in range(J_TILES)]
+
+        def load_a(u):
+            nc.sync.dma_start(
+                out=a_raw[u][:], in_=A_mid[HALF * u : HALF * (u + 1), :].rearrange("(p e) w -> p e w", e=2)
+            )
+
+        def load_h(b):
+            for s in range(W_PASSES):
+                for u in range(2):
+                    first = P * PACK * s + HALF * u
+                    nc.sync.dma_start(
+                        out=h_raw[b][s][:, 2 * u : 2 * u + 2, :],
+                        in_=h1[first : first + HALF, b, :].rearrange("(p e) c -> p e c", e=2),
+                    )
+
+        def load_w(jt):
+            nc.sync.dma_start(
+                out=w_raw[jt][:], in_=W1.rearrange("(v t p) c -> t p v c", v=2, p=P)[jt]
+            )
+
+        load_a(0)
+        load_h(0)
+        load_a(1)
+        for jt in range(J_TILES):
+            load_w(jt)
+        load_h(1)
+
+        bias = keep.tile([P, O // P], F32, name="bias")
+
+        def prepare_bias():
+            bias_ps = psum_t.tile([P, P], BF16, name="bias_ps", tag="t")
+            nc.tensor.transpose(out=bias_ps[:], in_=bias_rows[:], identity=ident_bf16[:])
+            nc.vector.tensor_copy(out=bias[:], in_=bias_ps[:, 0 : O // P])
+
+        a_codes = [keep.tile([P, W_PASSES, HALF], U32, name="a_codes%d" % u, align_bytes=64) for u in range(2)]
+        a_scales = [keep.tile([P, W_PASSES, HALF], U8, name="a_scales%d" % u, align_bytes=64) for u in range(2)]
+
+        def prepare_a(u):
+            for s in range(W_PASSES):
+                a_ps = psum_t.tile([P, 2, HALF], F32, name="a_ps", tag="t")
+                for e in range(2):
+                    words = a_raw[u][:, e, :].bitcast(F32)
+                    for uw in range(2):
+                        first = HALF * s + P * uw
+                        nc.tensor.transpose(
+                            out=a_ps[:, uw, P * e : P * (e + 1)], in_=words[:, first : first + P], identity=ident_f32[:]
+                        )
+                a_grouped = keep.tile([P, HALF, PACK], BF16, name="a_grouped%d_%d" % (u, s), align_bytes=64)
+                nc.scalar.copy(out=a_grouped[:].bitcast(F32), in_=a_ps[:].rearrange("p u i -> p i u"))
+                nc.vector.quantize_mx(
+                    out=a_codes[u][:, s, :].bitcast(FP8X4),
+                    scales=a_scales[u][:, s, :],
+                    in_=a_grouped[:].rearrange("p i t -> p (i t)"),
+                )
+
+        h_codes = [[keep.tile([P, C], U32, name="h_codes%d_%d" % (b, s), align_bytes=64) for s in range(W_PASSES)] for b in range(B)]
+        h_scales = [[keep.tile([P, C], U8, name="h_scales%d_%d" % (b, s), align_bytes=64) for s in range(W_PASSES)] for b in range(B)]
+
+        def prepare_h(b):
+            for s in range(W_PASSES):
+                h_grouped = keep.tile([P, C, PACK], BF16, name="h_grouped%d_%d" % (b, s), align_bytes=64)
+                src = h_raw[b][s][:].rearrange("p t (u q e) -> p u e q t", u=2, e=2)
+                dst = h_grouped[:].rearrange("p (u e q) t -> p u e q t", u=2, e=2)
+                nc.vector.tensor_copy(out=dst[:, 0], in_=src[:, 0])
+                nc.scalar.copy(out=dst[:, 1], in_=src[:, 1])
+                nc.vector.quantize_mx(
+                    out=h_codes[b][s][:].bitcast(FP8X4),
+                    scales=h_scales[b][s][:],
+                    in_=h_grouped[:].rearrange("p c t -> p (c t)"),
+                )
+
+        w_codes = [keep.tile([P, 2 * P], U32, name="w_codes%d" % jt, align_bytes=64) for jt in range(J_TILES)]
+        w_scales = [keep.tile([P, 2 * P], U8, name="w_scales%d" % jt, align_bytes=64) for jt in range(J_TILES)]
+
+        def prepare_w(jt):
+            w_ps = psum_t.tile([P, 2, 2 * P], F32, name="w_ps", tag="t")
+            for v in range(2):
+                words = w_raw[jt][:, v, :].bitcast(F32)
+                for uc in range(2):
+                    nc.tensor.transpose(
+                        out=w_ps[:, uc, P * v : P * (v + 1)], in_=words[:, P * uc : P * (uc + 1)], identity=ident_f32[:]
+                    )
+            w_grouped = keep.tile([P, 2 * P, PACK], BF16, name="w_grouped%d" % jt, align_bytes=64)
+            nc.scalar.copy(out=w_grouped[:].bitcast(F32), in_=w_ps[:].rearrange("p u o -> p o u"))
+            nc.vector.quantize_mx(
+                out=w_codes[jt][:].bitcast(FP8X4),
+                scales=w_scales[jt][:],
+                in_=w_grouped[:].rearrange("p o t -> p (o t)"),
+            )
+
+        g_codes = [[keep.tile([P, HALF], U32, name="g_codes%d_%d" % (b, u), align_bytes=64) for u in range(2)] for b in range(B)]
+        g_scales = [[keep.tile([P, HALF], U8, name="g_scales%d_%d" % (b, u), align_bytes=64) for u in range(2)] for b in range(B)]
+
+        def first_matmul(b, u):
+            g_grouped = keep.tile([P, HALF, PACK], BF16, name="g_grouped%d_%d" % (b, u), align_bytes=64)
+            for e in range(2):
+                g_ps = psum_g.tile([P, PACK, P], F32, name="g_ps")
+                for t in range(PACK):
+                    for s in range(W_PASSES):
+                        nc.tensor.matmul_mx(
+                            out=g_ps[:, t, :],
+                            lhsT=h_codes[b][s][:, P * t : P * (t + 1)].bitcast(FP8X4),
+                            lhsT_scale=h_scales[b][s][:, P * t : P * (t + 1)],
+                            rhs=a_codes[u][:, s, P * e : P * (e + 1)].bitcast(FP8X4),
+                            rhs_scale=a_scales[u][:, s, P * e : P * (e + 1)],
+                            start=(s == 0),
+                            stop=(s == W_PASSES - 1),
+                        )
+                nc.scalar.copy(out=g_grouped[:, P * e : P * (e + 1), :], in_=g_ps[:].rearrange("p t i -> p i t"))
+            nc.vector.quantize_mx(
+                out=g_codes[b][u][:].bitcast(FP8X4),
+                scales=g_scales[b][u][:],
+                in_=g_grouped[:].rearrange("p i t -> p (i t)"),
+            )
+
+        out_sb = [keep.tile([P, PACK, C], F32, name="out_sb%d" % b) for b in range(B)]
+
+        def second_matmul(b, u):
+            for jp in range(J_TILES // 2):
+                o_ps = psum_t.tile([P, 2, 2 * P], F32, name="o_ps", tag="t")
+                for jl in range(2):
+                    jt = 2 * jp + jl
+                    y_ps = psum_y.tile([P, 2, HALF], F32, name="y_ps")
+                    for v in range(2):
+                        nc.tensor.matmul_mx(
+                            out=y_ps[:, v, :],
+                            lhsT=w_codes[jt][:, P * v : P * (v + 1)].bitcast(FP8X4),
+                            lhsT_scale=w_scales[jt][:, P * v : P * (v + 1)],
+                            rhs=g_codes[b][u][:].bitcast(FP8X4),
+                            rhs_scale=g_scales[b][u][:],
+                            start=True,
+                            stop=True,
+                        )
+                    gate = work.tile([P, HALF], F32, name="gate")
+                    nc.scalar.activation(
+                        out=gate[:], in_=y_ps[:, 1, :], func=ACT.Sigmoid, bias=bias[:, J_TILES + jt : J_TILES + jt + 1], scale=1.0
+                    )
+                    h2 = work.tile([P, HALF], F32, name="h2")
+                    nc.vector.scalar_tensor_tensor(
+                        out=h2[:], in0=y_ps[:, 0, :], scalar=bias[:, jt : jt + 1], in1=gate[:], op0=ALU.add, op1=ALU.mult
+                    )
+                    for e in range(2):
+                        nc.tensor.transpose(
+                            out=o_ps[:, e, P * jl : P * (jl + 1)], in_=h2[:, P * e : P * (e + 1)], identity=ident_f32[:]
+                        )
+                cols = slice(2 * P * jp, 2 * P * (jp + 1))
+                nc.vector.tensor_tensor(
+                    out=out_sb[b][:, 2 * u : 2 * u + 2, cols],
+                    in0=o_ps[:],
+                    in1=h_raw[b][1][:, 2 * u : 2 * u + 2, cols],
+                    op=ALU.max,
+                )
+            nc.sync.dma_start(
+                out=out[HALF * u : HALF * (u + 1), b, :].rearrange("(p e) j -> p e j", e=2),
+                in_=out_sb[b][:, 2 * u : 2 * u + 2, :],
+            )
+
+        prepare_a(0)
+        prepare_h(0)
+        first_matmul(0, 0)
+        prepare_a(1)
+        first_matmul(0, 1)
+        prepare_bias()
+        for jt in range(J_TILES):
+            prepare_w(jt)
+        second_matmul(0, 0)
+        second_matmul(0, 1)
+        prepare_h(1)
+        first_matmul(1, 0)
+        second_matmul(1, 0)
+        first_matmul(1, 1)
+        second_matmul(1, 1)

@@ -70,12 +70,12 @@ def tile_stsgcm_pb_kernel(tc, h1, A_mid, W1, b1, out):
                 out=w_raw[jt][:], in_=W1.rearrange("(v t p) c -> t p v c", v=2, p=P)[jt]
             )
 
-        load_a(0)
         load_h(0)
+        load_a(0)
         load_a(1)
+        load_h(1)
         for jt in range(J_TILES):
             load_w(jt)
-        load_h(1)
 
         bias = keep.tile([P, O // P], F32, name="bias")
 
@@ -207,18 +207,18 @@ def tile_stsgcm_pb_kernel(tc, h1, A_mid, W1, b1, out):
                 in_=out_sb[b][:, 2 * u : 2 * u + 2, :],
             )
 
-        prepare_a(0)
         prepare_h(0)
-        first_matmul(0, 0)
+        prepare_a(0)
         prepare_a(1)
-        first_matmul(0, 1)
+        first_matmul(0, 0)
+        prepare_h(1)
         prepare_bias()
         for jt in range(J_TILES):
             prepare_w(jt)
+        first_matmul(0, 1)
         second_matmul(0, 0)
-        second_matmul(0, 1)
-        prepare_h(1)
         first_matmul(1, 0)
-        second_matmul(1, 0)
+        second_matmul(0, 1)
         first_matmul(1, 1)
+        second_matmul(1, 0)
         second_matmul(1, 1)

@@ -29,10 +29,11 @@ def tile_stsgcm_pb_kernel(tc, h1, A_mid, W1, b1, out):
     nc = tc.nc
     with ExitStack() as stack:
         keep = stack.enter_context(tc.tile_pool(name="keep", bufs=1))
-        work = stack.enter_context(tc.tile_pool(name="work", bufs=4))
+        work = stack.enter_context(tc.tile_pool(name="work", bufs=8))
         psum_t = stack.enter_context(tc.psum_pool(name="psum_t", bufs=2))
         psum_g = stack.enter_context(tc.psum_pool(name="psum_g", bufs=2))
         psum_y = stack.enter_context(tc.psum_pool(name="psum_y", bufs=4))
+        stack.enter_context(tc.manual_schedule())
 
         ident_f32 = keep.tile([P, P], F32, name="ident_f32")
         nc.vector.memset(ident_f32[:], 0.0)
@@ -78,53 +79,62 @@ def tile_stsgcm_pb_kernel(tc, h1, A_mid, W1, b1, out):
             load_w(jt)
 
         bias = keep.tile([P, O // P], F32, name="bias")
+        a_codes = [keep.tile([P, W_PASSES, HALF], U32, name="a_codes%d" % u, align_bytes=64) for u in range(2)]
+        a_scales = [keep.tile([P, W_PASSES, HALF], U8, name="a_scales%d" % u, align_bytes=64) for u in range(2)]
+        h_codes = [[keep.tile([P, C], U32, name="h_codes%d_%d" % (b, s), align_bytes=64) for s in range(W_PASSES)] for b in range(B)]
+        h_scales = [[keep.tile([P, C], U8, name="h_scales%d_%d" % (b, s), align_bytes=64) for s in range(W_PASSES)] for b in range(B)]
+        w_codes = [keep.tile([P, 2 * P], U32, name="w_codes%d" % jt, align_bytes=64) for jt in range(J_TILES)]
+        w_scales = [keep.tile([P, 2 * P], U8, name="w_scales%d" % jt, align_bytes=64) for jt in range(J_TILES)]
+        g_codes = [[keep.tile([P, HALF], U32, name="g_codes%d_%d" % (b, u), align_bytes=64) for u in range(2)] for b in range(B)]
+        g_scales = [[keep.tile([P, HALF], U8, name="g_scales%d_%d" % (b, u), align_bytes=64) for u in range(2)] for b in range(B)]
+        a_grouped = [[keep.tile([P, HALF, PACK], BF16, name="a_grouped%d_%d" % (u, s), align_bytes=64) for s in range(W_PASSES)] for u in range(2)]
+        h_grouped = [[keep.tile([P, C, PACK], BF16, name="h_grouped%d_%d" % (b, s), align_bytes=64) for s in range(W_PASSES)] for b in range(B)]
+        w_grouped = [keep.tile([P, 2 * P, PACK], BF16, name="w_grouped%d" % jt, align_bytes=64) for jt in range(J_TILES)]
+        g_grouped = [[keep.tile([P, HALF, PACK], BF16, name="g_grouped%d_%d" % (b, u), align_bytes=64) for u in range(2)] for b in range(B)]
+        out_sb = [keep.tile([P, PACK, C], F32, name="out_sb%d" % b) for b in range(B)]
+        y_banks = {}
+        gates = {}
+        gated = {}
+        o_banks = {}
 
         def prepare_bias():
             bias_ps = psum_t.tile([P, P], BF16, name="bias_ps", tag="t")
             nc.tensor.transpose(out=bias_ps[:], in_=bias_rows[:], identity=ident_bf16[:])
             nc.vector.tensor_copy(out=bias[:], in_=bias_ps[:, 0 : O // P])
 
-        a_codes = [keep.tile([P, W_PASSES, HALF], U32, name="a_codes%d" % u, align_bytes=64) for u in range(2)]
-        a_scales = [keep.tile([P, W_PASSES, HALF], U8, name="a_scales%d" % u, align_bytes=64) for u in range(2)]
+        def transpose_a(u, s):
+            a_ps = psum_t.tile([P, 2, HALF], F32, name="a_ps", tag="t")
+            for e in range(2):
+                words = a_raw[u][:, e, :].bitcast(F32)
+                for uw in range(2):
+                    first = HALF * s + P * uw
+                    nc.tensor.transpose(
+                        out=a_ps[:, uw, P * e : P * (e + 1)], in_=words[:, first : first + P], identity=ident_f32[:]
+                    )
+            nc.scalar.copy(out=a_grouped[u][s][:].bitcast(F32), in_=a_ps[:].rearrange("p u i -> p i u"))
 
-        def prepare_a(u):
-            for s in range(W_PASSES):
-                a_ps = psum_t.tile([P, 2, HALF], F32, name="a_ps", tag="t")
-                for e in range(2):
-                    words = a_raw[u][:, e, :].bitcast(F32)
-                    for uw in range(2):
-                        first = HALF * s + P * uw
-                        nc.tensor.transpose(
-                            out=a_ps[:, uw, P * e : P * (e + 1)], in_=words[:, first : first + P], identity=ident_f32[:]
-                        )
-                a_grouped = keep.tile([P, HALF, PACK], BF16, name="a_grouped%d_%d" % (u, s), align_bytes=64)
-                nc.scalar.copy(out=a_grouped[:].bitcast(F32), in_=a_ps[:].rearrange("p u i -> p i u"))
-                nc.vector.quantize_mx(
-                    out=a_codes[u][:, s, :].bitcast(FP8X4),
-                    scales=a_scales[u][:, s, :],
-                    in_=a_grouped[:].rearrange("p i t -> p (i t)"),
-                )
+        def quantise_a(u, s):
+            nc.vector.quantize_mx(
+                out=a_codes[u][:, s, :].bitcast(FP8X4),
+                scales=a_scales[u][:, s, :],
+                in_=a_grouped[u][s][:].rearrange("p i t -> p (i t)"),
+            )
 
-        h_codes = [[keep.tile([P, C], U32, name="h_codes%d_%d" % (b, s), align_bytes=64) for s in range(W_PASSES)] for b in range(B)]
-        h_scales = [[keep.tile([P, C], U8, name="h_scales%d_%d" % (b, s), align_bytes=64) for s in range(W_PASSES)] for b in range(B)]
+        def regroup_h(b, s):
+            src = h_raw[b][s][:].rearrange("p t (u q e) -> p u e q t", u=2, e=2)
+            dst = h_grouped[b][s][:].rearrange("p (u e q) t -> p u e q t", u=2, e=2)
+            nc.vector.tensor_copy(out=dst[:, 0], in_=src[:, 0])
+            nc.vector.tensor_copy(out=dst[:, 1, 0], in_=src[:, 1, 0])
+            nc.scalar.copy(out=dst[:, 1, 1], in_=src[:, 1, 1])
 
-        def prepare_h(b):
-            for s in range(W_PASSES):
-                h_grouped = keep.tile([P, C, PACK], BF16, name="h_grouped%d_%d" % (b, s), align_bytes=64)
-                src = h_raw[b][s][:].rearrange("p t (u q e) -> p u e q t", u=2, e=2)
-                dst = h_grouped[:].rearrange("p (u e q) t -> p u e q t", u=2, e=2)
-                nc.vector.tensor_copy(out=dst[:, 0], in_=src[:, 0])
-                nc.scalar.copy(out=dst[:, 1], in_=src[:, 1])
-                nc.vector.quantize_mx(
-                    out=h_codes[b][s][:].bitcast(FP8X4),
-                    scales=h_scales[b][s][:],
-                    in_=h_grouped[:].rearrange("p c t -> p (c t)"),
-                )
+        def quantise_h(b, s):
+            nc.vector.quantize_mx(
+                out=h_codes[b][s][:].bitcast(FP8X4),
+                scales=h_scales[b][s][:],
+                in_=h_grouped[b][s][:].rearrange("p c t -> p (c t)"),
+            )
 
-        w_codes = [keep.tile([P, 2 * P], U32, name="w_codes%d" % jt, align_bytes=64) for jt in range(J_TILES)]
-        w_scales = [keep.tile([P, 2 * P], U8, name="w_scales%d" % jt, align_bytes=64) for jt in range(J_TILES)]
-
-        def prepare_w(jt):
+        def transpose_w(jt):
             w_ps = psum_t.tile([P, 2, 2 * P], F32, name="w_ps", tag="t")
             for v in range(2):
                 words = w_raw[jt][:, v, :].bitcast(F32)
@@ -132,93 +142,143 @@ def tile_stsgcm_pb_kernel(tc, h1, A_mid, W1, b1, out):
                     nc.tensor.transpose(
                         out=w_ps[:, uc, P * v : P * (v + 1)], in_=words[:, P * uc : P * (uc + 1)], identity=ident_f32[:]
                     )
-            w_grouped = keep.tile([P, 2 * P, PACK], BF16, name="w_grouped%d" % jt, align_bytes=64)
-            nc.scalar.copy(out=w_grouped[:].bitcast(F32), in_=w_ps[:].rearrange("p u o -> p o u"))
+            nc.scalar.copy(out=w_grouped[jt][:].bitcast(F32), in_=w_ps[:].rearrange("p u o -> p o u"))
+
+        def quantise_w(jt):
             nc.vector.quantize_mx(
                 out=w_codes[jt][:].bitcast(FP8X4),
                 scales=w_scales[jt][:],
-                in_=w_grouped[:].rearrange("p o t -> p (o t)"),
+                in_=w_grouped[jt][:].rearrange("p o t -> p (o t)"),
             )
 
-        g_codes = [[keep.tile([P, HALF], U32, name="g_codes%d_%d" % (b, u), align_bytes=64) for u in range(2)] for b in range(B)]
-        g_scales = [[keep.tile([P, HALF], U8, name="g_scales%d_%d" % (b, u), align_bytes=64) for u in range(2)] for b in range(B)]
+        def first_matmul(b, u, e):
+            g_ps = psum_g.tile([P, PACK, P], F32, name="g_ps")
+            for t in range(PACK):
+                for s in range(W_PASSES):
+                    nc.tensor.matmul_mx(
+                        out=g_ps[:, t, :],
+                        lhsT=h_codes[b][s][:, P * t : P * (t + 1)].bitcast(FP8X4),
+                        lhsT_scale=h_scales[b][s][:, P * t : P * (t + 1)],
+                        rhs=a_codes[u][:, s, P * e : P * (e + 1)].bitcast(FP8X4),
+                        rhs_scale=a_scales[u][:, s, P * e : P * (e + 1)],
+                        start=(s == 0),
+                        stop=(s == W_PASSES - 1),
+                    )
+            nc.scalar.copy(out=g_grouped[b][u][:, P * e : P * (e + 1), :], in_=g_ps[:].rearrange("p t i -> p i t"))
 
-        def first_matmul(b, u):
-            g_grouped = keep.tile([P, HALF, PACK], BF16, name="g_grouped%d_%d" % (b, u), align_bytes=64)
-            for e in range(2):
-                g_ps = psum_g.tile([P, PACK, P], F32, name="g_ps")
-                for t in range(PACK):
-                    for s in range(W_PASSES):
-                        nc.tensor.matmul_mx(
-                            out=g_ps[:, t, :],
-                            lhsT=h_codes[b][s][:, P * t : P * (t + 1)].bitcast(FP8X4),
-                            lhsT_scale=h_scales[b][s][:, P * t : P * (t + 1)],
-                            rhs=a_codes[u][:, s, P * e : P * (e + 1)].bitcast(FP8X4),
-                            rhs_scale=a_scales[u][:, s, P * e : P * (e + 1)],
-                            start=(s == 0),
-                            stop=(s == W_PASSES - 1),
-                        )
-                nc.scalar.copy(out=g_grouped[:, P * e : P * (e + 1), :], in_=g_ps[:].rearrange("p t i -> p i t"))
+        def quantise_g(b, u):
             nc.vector.quantize_mx(
                 out=g_codes[b][u][:].bitcast(FP8X4),
                 scales=g_scales[b][u][:],
-                in_=g_grouped[:].rearrange("p i t -> p (i t)"),
+                in_=g_grouped[b][u][:].rearrange("p i t -> p (i t)"),
             )
 
-        out_sb = [keep.tile([P, PACK, C], F32, name="out_sb%d" % b) for b in range(B)]
-
         def second_matmul(b, u):
+            for jt in range(J_TILES):
+                y_ps = psum_y.tile([P, 2, HALF], F32, name="y_ps")
+                y_banks[(b, u, jt)] = y_ps
+                for v in range(2):
+                    nc.tensor.matmul_mx(
+                        out=y_ps[:, v, :],
+                        lhsT=w_codes[jt][:, P * v : P * (v + 1)].bitcast(FP8X4),
+                        lhsT_scale=w_scales[jt][:, P * v : P * (v + 1)],
+                        rhs=g_codes[b][u][:].bitcast(FP8X4),
+                        rhs_scale=g_scales[b][u][:],
+                        start=True,
+                        stop=True,
+                    )
+                gate = work.tile([P, HALF], F32, name="gate")
+                gates[(b, u, jt)] = gate
+                nc.scalar.activation(
+                    out=gate[:], in_=y_ps[:, 1, :], func=ACT.Sigmoid, bias=bias[:, J_TILES + jt : J_TILES + jt + 1], scale=1.0
+                )
+
+        def apply_gate(b, u):
+            for jt in range(J_TILES):
+                h2 = work.tile([P, HALF], F32, name="h2")
+                gated[(b, u, jt)] = h2
+                nc.vector.scalar_tensor_tensor(
+                    out=h2[:], in0=y_banks[(b, u, jt)][:, 0, :], scalar=bias[:, jt : jt + 1], in1=gates[(b, u, jt)][:],
+                    op0=ALU.add, op1=ALU.mult,
+                )
+
+        def transpose_back(b, u):
             for jp in range(J_TILES // 2):
                 o_ps = psum_t.tile([P, 2, 2 * P], F32, name="o_ps", tag="t")
+                o_banks[(b, u, jp)] = o_ps
                 for jl in range(2):
-                    jt = 2 * jp + jl
-                    y_ps = psum_y.tile([P, 2, HALF], F32, name="y_ps")
-                    for v in range(2):
-                        nc.tensor.matmul_mx(
-                            out=y_ps[:, v, :],
-                            lhsT=w_codes[jt][:, P * v : P * (v + 1)].bitcast(FP8X4),
-                            lhsT_scale=w_scales[jt][:, P * v : P * (v + 1)],
-                            rhs=g_codes[b][u][:].bitcast(FP8X4),
-                            rhs_scale=g_scales[b][u][:],
-                            start=True,
-                            stop=True,
-                        )
-                    gate = work.tile([P, HALF], F32, name="gate")
-                    nc.scalar.activation(
-                        out=gate[:], in_=y_ps[:, 1, :], func=ACT.Sigmoid, bias=bias[:, J_TILES + jt : J_TILES + jt + 1], scale=1.0
-                    )
-                    h2 = work.tile([P, HALF], F32, name="h2")
-                    nc.vector.scalar_tensor_tensor(
-                        out=h2[:], in0=y_ps[:, 0, :], scalar=bias[:, jt : jt + 1], in1=gate[:], op0=ALU.add, op1=ALU.mult
-                    )
                     for e in range(2):
                         nc.tensor.transpose(
-                            out=o_ps[:, e, P * jl : P * (jl + 1)], in_=h2[:, P * e : P * (e + 1)], identity=ident_f32[:]
+                            out=o_ps[:, e, P * jl : P * (jl + 1)],
+                            in_=gated[(b, u, 2 * jp + jl)][:, P * e : P * (e + 1)],
+                            identity=ident_f32[:],
                         )
+
+        def take_max(b, u):
+            for jp in range(J_TILES // 2):
                 cols = slice(2 * P * jp, 2 * P * (jp + 1))
                 nc.vector.tensor_tensor(
                     out=out_sb[b][:, 2 * u : 2 * u + 2, cols],
-                    in0=o_ps[:],
+                    in0=o_banks[(b, u, jp)][:],
                     in1=h_raw[b][1][:, 2 * u : 2 * u + 2, cols],
                     op=ALU.max,
                 )
-            nc.sync.dma_start(
-                out=out[HALF * u : HALF * (u + 1), b, :].rearrange("(p e) j -> p e j", e=2),
-                in_=out_sb[b][:, 2 * u : 2 * u + 2, :],
-            )
+                nc.sync.dma_start(
+                    out=out[HALF * u : HALF * (u + 1), b, cols].rearrange("(p e) j -> p e j", e=2),
+                    in_=out_sb[b][:, 2 * u : 2 * u + 2, cols],
+                )
 
-        prepare_h(0)
-        prepare_a(0)
-        prepare_a(1)
-        first_matmul(0, 0)
-        prepare_h(1)
+        for s in range(W_PASSES):
+            regroup_h(0, s)
+            if s > 0:
+                quantise_h(0, s - 1)
+        quantise_h(0, W_PASSES - 1)
+        for u in range(2):
+            for s in range(W_PASSES):
+                transpose_a(u, s)
+                if s > 0:
+                    quantise_a(u, s - 1)
+            quantise_a(u, W_PASSES - 1)
+        regroup_h(1, 0)
+        first_matmul(0, 0, 0)
+        regroup_h(1, 1)
+        quantise_h(1, 0)
+        first_matmul(0, 0, 1)
+        regroup_h(1, 2)
+        quantise_h(1, 1)
+        quantise_h(1, 2)
         prepare_bias()
-        for jt in range(J_TILES):
-            prepare_w(jt)
-        first_matmul(0, 1)
+        transpose_w(0)
+        transpose_w(1)
+        quantise_g(0, 0)
+        first_matmul(0, 1, 0)
+        first_matmul(0, 1, 1)
+        quantise_w(0)
+        quantise_w(1)
+        transpose_w(2)
+        transpose_w(3)
+        quantise_g(0, 1)
+        quantise_w(2)
+        quantise_w(3)
+        first_matmul(1, 0, 0)
+        first_matmul(1, 0, 1)
         second_matmul(0, 0)
-        first_matmul(1, 0)
+        quantise_g(1, 0)
+        apply_gate(0, 0)
+        first_matmul(1, 1, 0)
+        first_matmul(1, 1, 1)
+        transpose_back(0, 0)
         second_matmul(0, 1)
-        first_matmul(1, 1)
+        quantise_g(1, 1)
+        take_max(0, 0)
+        apply_gate(0, 1)
+        transpose_back(0, 1)
         second_matmul(1, 0)
+        take_max(0, 1)
+        apply_gate(1, 0)
+        transpose_back(1, 0)
         second_matmul(1, 1)
+        take_max(1, 0)
+        apply_gate(1, 1)
+        transpose_back(1, 1)
+        take_max(1, 1)

@@ -21,6 +21,7 @@ O = 2 * C
 W_PASSES = N_SOURCE // (P * PACK)
 HALF = 256
 J_TILES = C // P
+RUN = 4
 
 FLOPS = 2 * B * C * N_TARGET * N_SOURCE + 2 * B * O * C * N_TARGET
 
@@ -29,12 +30,14 @@ def tile_stsgcm_pb_kernel(tc, h1, A_mid, W1, b1, out):
     nc = tc.nc
     with ExitStack() as stack:
         keep = stack.enter_context(tc.tile_pool(name="keep", bufs=1))
-        work = stack.enter_context(tc.tile_pool(name="work", bufs=8))
+        work = stack.enter_context(tc.tile_pool(name="work", bufs=4))
         psum_t = stack.enter_context(tc.psum_pool(name="psum_t", bufs=2))
         psum_g = stack.enter_context(tc.psum_pool(name="psum_g", bufs=2))
         psum_y = stack.enter_context(tc.psum_pool(name="psum_y", bufs=4))
-        stack.enter_context(tc.manual_schedule())
 
+        bias_rows = keep.tile([P, P], BF16, name="bias_rows")
+        nc.vector.memset(bias_rows[:], 0.0)
+        nc.sync.dma_start(out=bias_rows[0 : O // P, :], in_=b1.rearrange("(t p) -> t p", p=P))
         ident_f32 = keep.tile([P, P], F32, name="ident_f32")
         nc.vector.memset(ident_f32[:], 0.0)
         make_identity(nc, ident_f32[:], nomemset=True)
@@ -44,9 +47,6 @@ def tile_stsgcm_pb_kernel(tc, h1, A_mid, W1, b1, out):
         warm_out = keep.tile([P, 1], F32, name="warm_out")
         nc.vector.memset(warm_in[:], 0.0)
         nc.scalar.activation(out=warm_out[:], in_=warm_in[:], func=ACT.Sigmoid)
-        bias_rows = keep.tile([P, P], BF16, name="bias_rows")
-        nc.vector.memset(bias_rows[:], 0.0)
-        nc.scalar.dma_start(out=bias_rows[0 : O // P, :], in_=b1.rearrange("(t p) -> t p", p=P))
 
         a_raw = [keep.tile([P, 2, N_SOURCE], BF16, name="a_raw%d" % u) for u in range(2)]
         h_raw = [[keep.tile([P, PACK, C], BF16, name="h_raw%d_%d" % (b, s)) for s in range(W_PASSES)] for b in range(B)]
@@ -79,62 +79,54 @@ def tile_stsgcm_pb_kernel(tc, h1, A_mid, W1, b1, out):
             load_w(jt)
 
         bias = keep.tile([P, O // P], F32, name="bias")
-        a_codes = [keep.tile([P, W_PASSES, HALF], U32, name="a_codes%d" % u, align_bytes=64) for u in range(2)]
-        a_scales = [keep.tile([P, W_PASSES, HALF], U8, name="a_scales%d" % u, align_bytes=64) for u in range(2)]
-        h_codes = [[keep.tile([P, C], U32, name="h_codes%d_%d" % (b, s), align_bytes=64) for s in range(W_PASSES)] for b in range(B)]
-        h_scales = [[keep.tile([P, C], U8, name="h_scales%d_%d" % (b, s), align_bytes=64) for s in range(W_PASSES)] for b in range(B)]
-        w_codes = [keep.tile([P, 2 * P], U32, name="w_codes%d" % jt, align_bytes=64) for jt in range(J_TILES)]
-        w_scales = [keep.tile([P, 2 * P], U8, name="w_scales%d" % jt, align_bytes=64) for jt in range(J_TILES)]
-        g_codes = [[keep.tile([P, HALF], U32, name="g_codes%d_%d" % (b, u), align_bytes=64) for u in range(2)] for b in range(B)]
-        g_scales = [[keep.tile([P, HALF], U8, name="g_scales%d_%d" % (b, u), align_bytes=64) for u in range(2)] for b in range(B)]
-        a_grouped = [[keep.tile([P, HALF, PACK], BF16, name="a_grouped%d_%d" % (u, s), align_bytes=64) for s in range(W_PASSES)] for u in range(2)]
-        h_grouped = [[keep.tile([P, C, PACK], BF16, name="h_grouped%d_%d" % (b, s), align_bytes=64) for s in range(W_PASSES)] for b in range(B)]
-        w_grouped = [keep.tile([P, 2 * P, PACK], BF16, name="w_grouped%d" % jt, align_bytes=64) for jt in range(J_TILES)]
-        g_grouped = [[keep.tile([P, HALF, PACK], BF16, name="g_grouped%d_%d" % (b, u), align_bytes=64) for u in range(2)] for b in range(B)]
-        out_sb = [keep.tile([P, PACK, C], F32, name="out_sb%d" % b) for b in range(B)]
-        y_banks = {}
-        gates = {}
-        gated = {}
-        o_banks = {}
 
         def prepare_bias():
             bias_ps = psum_t.tile([P, P], BF16, name="bias_ps", tag="t")
             nc.tensor.transpose(out=bias_ps[:], in_=bias_rows[:], identity=ident_bf16[:])
             nc.vector.tensor_copy(out=bias[:], in_=bias_ps[:, 0 : O // P])
 
-        def transpose_a(u, s):
-            a_ps = psum_t.tile([P, 2, HALF], F32, name="a_ps", tag="t")
-            for e in range(2):
-                words = a_raw[u][:, e, :].bitcast(F32)
-                for uw in range(2):
-                    first = HALF * s + P * uw
-                    nc.tensor.transpose(
-                        out=a_ps[:, uw, P * e : P * (e + 1)], in_=words[:, first : first + P], identity=ident_f32[:]
-                    )
-            nc.scalar.copy(out=a_grouped[u][s][:].bitcast(F32), in_=a_ps[:].rearrange("p u i -> p i u"))
+        a_codes = [keep.tile([P, W_PASSES, HALF], U32, name="a_codes%d" % u, align_bytes=64) for u in range(2)]
+        a_scales = [keep.tile([P, W_PASSES, HALF], U8, name="a_scales%d" % u, align_bytes=64) for u in range(2)]
 
-        def quantise_a(u, s):
-            nc.vector.quantize_mx(
-                out=a_codes[u][:, s, :].bitcast(FP8X4),
-                scales=a_scales[u][:, s, :],
-                in_=a_grouped[u][s][:].rearrange("p i t -> p (i t)"),
-            )
+        def prepare_a(u):
+            for s in range(W_PASSES):
+                a_ps = psum_t.tile([P, 2, HALF], F32, name="a_ps", tag="t")
+                for e in range(2):
+                    words = a_raw[u][:, e, :].bitcast(F32)
+                    for uw in range(2):
+                        first = HALF * s + P * uw
+                        nc.tensor.transpose(
+                            out=a_ps[:, uw, P * e : P * (e + 1)], in_=words[:, first : first + P], identity=ident_f32[:]
+                        )
+                a_grouped = keep.tile([P, HALF, PACK], BF16, name="a_grouped%d_%d" % (u, s), align_bytes=64)
+                nc.scalar.copy(out=a_grouped[:].bitcast(F32), in_=a_ps[:].rearrange("p u i -> p i u"))
+                nc.vector.quantize_mx(
+                    out=a_codes[u][:, s, :].bitcast(FP8X4),
+                    scales=a_scales[u][:, s, :],
+                    in_=a_grouped[:].rearrange("p i t -> p (i t)"),
+                )
 
-        def regroup_h(b, s):
-            src = h_raw[b][s][:].rearrange("p t (u q e) -> p u e q t", u=2, e=2)
-            dst = h_grouped[b][s][:].rearrange("p (u e q) t -> p u e q t", u=2, e=2)
-            nc.vector.tensor_copy(out=dst[:, 0], in_=src[:, 0])
-            nc.vector.tensor_copy(out=dst[:, 1, 0], in_=src[:, 1, 0])
-            nc.scalar.copy(out=dst[:, 1, 1], in_=src[:, 1, 1])
+        h_codes = [[keep.tile([P, C], U32, name="h_codes%d_%d" % (b, s), align_bytes=64) for s in range(W_PASSES)] for b in range(B)]
+        h_scales = [[keep.tile([P, C], U8, name="h_scales%d_%d" % (b, s), align_bytes=64) for s in range(W_PASSES)] for b in range(B)]
 
-        def quantise_h(b, s):
-            nc.vector.quantize_mx(
-                out=h_codes[b][s][:].bitcast(FP8X4),
-                scales=h_scales[b][s][:],
-                in_=h_grouped[b][s][:].rearrange("p c t -> p (c t)"),
-            )
+        def prepare_h(b):
+            for s in range(W_PASSES):
+                h_grouped = keep.tile([P, C, PACK], BF16, name="h_grouped%d_%d" % (b, s), align_bytes=64)
+                src = h_raw[b][s][:].rearrange("p t (u q i e) -> p u e q t i", u=2, i=RUN, e=2)
+                dst = h_grouped[:].rearrange("p (u e q i) t -> p u e q t i", u=2, e=2, i=RUN)
+                for e in range(2):
+                    nc.vector.tensor_copy(out=dst[:, 0, e], in_=src[:, 0, e])
+                    nc.scalar.copy(out=dst[:, 1, e], in_=src[:, 1, e])
+                nc.vector.quantize_mx(
+                    out=h_codes[b][s][:].bitcast(FP8X4),
+                    scales=h_scales[b][s][:],
+                    in_=h_grouped[:].rearrange("p c t -> p (c t)"),
+                )
 
-        def transpose_w(jt):
+        w_codes = [keep.tile([P, 2 * P], U32, name="w_codes%d" % jt, align_bytes=64) for jt in range(J_TILES)]
+        w_scales = [keep.tile([P, 2 * P], U8, name="w_scales%d" % jt, align_bytes=64) for jt in range(J_TILES)]
+
+        def prepare_w(jt):
             w_ps = psum_t.tile([P, 2, 2 * P], F32, name="w_ps", tag="t")
             for v in range(2):
                 words = w_raw[jt][:, v, :].bitcast(F32)
@@ -142,84 +134,73 @@ def tile_stsgcm_pb_kernel(tc, h1, A_mid, W1, b1, out):
                     nc.tensor.transpose(
                         out=w_ps[:, uc, P * v : P * (v + 1)], in_=words[:, P * uc : P * (uc + 1)], identity=ident_f32[:]
                     )
-            nc.scalar.copy(out=w_grouped[jt][:].bitcast(F32), in_=w_ps[:].rearrange("p u o -> p o u"))
-
-        def quantise_w(jt):
+            w_grouped = keep.tile([P, 2 * P, PACK], BF16, name="w_grouped%d" % jt, align_bytes=64)
+            nc.scalar.copy(out=w_grouped[:].bitcast(F32), in_=w_ps[:].rearrange("p u o -> p o u"))
             nc.vector.quantize_mx(
                 out=w_codes[jt][:].bitcast(FP8X4),
                 scales=w_scales[jt][:],
-                in_=w_grouped[jt][:].rearrange("p o t -> p (o t)"),
+                in_=w_grouped[:].rearrange("p o t -> p (o t)"),
             )
 
-        def first_matmul(b, u, e):
-            g_ps = psum_g.tile([P, PACK, P], F32, name="g_ps")
-            for t in range(PACK):
-                for s in range(W_PASSES):
-                    nc.tensor.matmul_mx(
-                        out=g_ps[:, t, :],
-                        lhsT=h_codes[b][s][:, P * t : P * (t + 1)].bitcast(FP8X4),
-                        lhsT_scale=h_scales[b][s][:, P * t : P * (t + 1)],
-                        rhs=a_codes[u][:, s, P * e : P * (e + 1)].bitcast(FP8X4),
-                        rhs_scale=a_scales[u][:, s, P * e : P * (e + 1)],
-                        start=(s == 0),
-                        stop=(s == W_PASSES - 1),
-                    )
-            nc.scalar.copy(out=g_grouped[b][u][:, P * e : P * (e + 1), :], in_=g_ps[:].rearrange("p t i -> p i t"))
+        g_codes = [[keep.tile([P, HALF], U32, name="g_codes%d_%d" % (b, u), align_bytes=64) for u in range(2)] for b in range(B)]
+        g_scales = [[keep.tile([P, HALF], U8, name="g_scales%d_%d" % (b, u), align_bytes=64) for u in range(2)] for b in range(B)]
 
-        def quantise_g(b, u):
+        def first_matmul(b, u):
+            g_grouped = keep.tile([P, HALF, PACK], BF16, name="g_grouped%d_%d" % (b, u), align_bytes=64)
+            for e in range(2):
+                g_ps = psum_g.tile([P, PACK, P], F32, name="g_ps")
+                for t in range(PACK):
+                    for s in range(W_PASSES):
+                        nc.tensor.matmul_mx(
+                            out=g_ps[:, t, :],
+                            lhsT=h_codes[b][s][:, P * t : P * (t + 1)].bitcast(FP8X4),
+                            lhsT_scale=h_scales[b][s][:, P * t : P * (t + 1)],
+                            rhs=a_codes[u][:, s, P * e : P * (e + 1)].bitcast(FP8X4),
+                            rhs_scale=a_scales[u][:, s, P * e : P * (e + 1)],
+                            start=(s == 0),
+                            stop=(s == W_PASSES - 1),
+                        )
+                nc.scalar.copy(out=g_grouped[:, P * e : P * (e + 1), :], in_=g_ps[:].rearrange("p t i -> p i t"))
             nc.vector.quantize_mx(
                 out=g_codes[b][u][:].bitcast(FP8X4),
                 scales=g_scales[b][u][:],
-                in_=g_grouped[b][u][:].rearrange("p i t -> p (i t)"),
+                in_=g_grouped[:].rearrange("p i t -> p (i t)"),
             )
 
+        out_sb = [keep.tile([P, PACK, C], F32, name="out_sb%d" % b) for b in range(B)]
+
         def second_matmul(b, u):
-            for jt in range(J_TILES):
-                y_ps = psum_y.tile([P, 2, HALF], F32, name="y_ps")
-                y_banks[(b, u, jt)] = y_ps
-                for v in range(2):
-                    nc.tensor.matmul_mx(
-                        out=y_ps[:, v, :],
-                        lhsT=w_codes[jt][:, P * v : P * (v + 1)].bitcast(FP8X4),
-                        lhsT_scale=w_scales[jt][:, P * v : P * (v + 1)],
-                        rhs=g_codes[b][u][:].bitcast(FP8X4),
-                        rhs_scale=g_scales[b][u][:],
-                        start=True,
-                        stop=True,
-                    )
-                gate = work.tile([P, HALF], F32, name="gate")
-                gates[(b, u, jt)] = gate
-                nc.scalar.activation(
-                    out=gate[:], in_=y_ps[:, 1, :], func=ACT.Sigmoid, bias=bias[:, J_TILES + jt : J_TILES + jt + 1], scale=1.0
-                )
-
-        def apply_gate(b, u):
-            for jt in range(J_TILES):
-                h2 = work.tile([P, HALF], F32, name="h2")
-                gated[(b, u, jt)] = h2
-                nc.vector.scalar_tensor_tensor(
-                    out=h2[:], in0=y_banks[(b, u, jt)][:, 0, :], scalar=bias[:, jt : jt + 1], in1=gates[(b, u, jt)][:],
-                    op0=ALU.add, op1=ALU.mult,
-                )
-
-        def transpose_back(b, u):
             for jp in range(J_TILES // 2):
                 o_ps = psum_t.tile([P, 2, 2 * P], F32, name="o_ps", tag="t")
-                o_banks[(b, u, jp)] = o_ps
                 for jl in range(2):
+                    jt = 2 * jp + jl
+                    y_ps = psum_y.tile([P, 2, HALF], F32, name="y_ps")
+                    for v in range(2):
+                        nc.tensor.matmul_mx(
+                            out=y_ps[:, v, :],
+                            lhsT=w_codes[jt][:, P * v : P * (v + 1)].bitcast(FP8X4),
+                            lhsT_scale=w_scales[jt][:, P * v : P * (v + 1)],
+                            rhs=g_codes[b][u][:].bitcast(FP8X4),
+                            rhs_scale=g_scales[b][u][:],
+                            start=True,
+                            stop=True,
+                        )
+                    gate = work.tile([P, HALF], F32, name="gate")
+                    nc.scalar.activation(
+                        out=gate[:], in_=y_ps[:, 1, :], func=ACT.Sigmoid, bias=bias[:, J_TILES + jt : J_TILES + jt + 1], scale=1.0
+                    )
+                    h2 = work.tile([P, HALF], F32, name="h2")
+                    nc.vector.scalar_tensor_tensor(
+                        out=h2[:], in0=y_ps[:, 0, :], scalar=bias[:, jt : jt + 1], in1=gate[:], op0=ALU.add, op1=ALU.mult
+                    )
                     for e in range(2):
                         nc.tensor.transpose(
-                            out=o_ps[:, e, P * jl : P * (jl + 1)],
-                            in_=gated[(b, u, 2 * jp + jl)][:, P * e : P * (e + 1)],
-                            identity=ident_f32[:],
+                            out=o_ps[:, e, P * jl : P * (jl + 1)], in_=h2[:, P * e : P * (e + 1)], identity=ident_f32[:]
                         )
-
-        def take_max(b, u):
-            for jp in range(J_TILES // 2):
                 cols = slice(2 * P * jp, 2 * P * (jp + 1))
                 nc.vector.tensor_tensor(
                     out=out_sb[b][:, 2 * u : 2 * u + 2, cols],
-                    in0=o_banks[(b, u, jp)][:],
+                    in0=o_ps[:],
                     in1=h_raw[b][1][:, 2 * u : 2 * u + 2, cols],
                     op=ALU.max,
                 )
@@ -228,57 +209,18 @@ def tile_stsgcm_pb_kernel(tc, h1, A_mid, W1, b1, out):
                     in_=out_sb[b][:, 2 * u : 2 * u + 2, cols],
                 )
 
-        for s in range(W_PASSES):
-            regroup_h(0, s)
-            if s > 0:
-                quantise_h(0, s - 1)
-        quantise_h(0, W_PASSES - 1)
-        for u in range(2):
-            for s in range(W_PASSES):
-                transpose_a(u, s)
-                if s > 0:
-                    quantise_a(u, s - 1)
-            quantise_a(u, W_PASSES - 1)
-        regroup_h(1, 0)
-        first_matmul(0, 0, 0)
-        regroup_h(1, 1)
-        quantise_h(1, 0)
-        first_matmul(0, 0, 1)
-        regroup_h(1, 2)
-        quantise_h(1, 1)
-        quantise_h(1, 2)
+        prepare_h(0)
+        prepare_a(0)
+        prepare_a(1)
+        first_matmul(0, 0)
+        prepare_h(1)
         prepare_bias()
-        transpose_w(0)
-        transpose_w(1)
-        quantise_g(0, 0)
-        first_matmul(0, 1, 0)
-        first_matmul(0, 1, 1)
-        quantise_w(0)
-        quantise_w(1)
-        transpose_w(2)
-        transpose_w(3)
-        quantise_g(0, 1)
-        quantise_w(2)
-        quantise_w(3)
-        first_matmul(1, 0, 0)
-        first_matmul(1, 0, 1)
+        for jt in range(J_TILES):
+            prepare_w(jt)
+        first_matmul(0, 1)
         second_matmul(0, 0)
-        quantise_g(1, 0)
-        apply_gate(0, 0)
-        first_matmul(1, 1, 0)
-        first_matmul(1, 1, 1)
-        transpose_back(0, 0)
+        first_matmul(1, 0)
         second_matmul(0, 1)
-        quantise_g(1, 1)
-        take_max(0, 0)
-        apply_gate(0, 1)
-        transpose_back(0, 1)
+        first_matmul(1, 1)
         second_matmul(1, 0)
-        take_max(0, 1)
-        apply_gate(1, 0)
-        transpose_back(1, 0)
         second_matmul(1, 1)
-        take_max(1, 0)
-        apply_gate(1, 1)
-        transpose_back(1, 1)
-        take_max(1, 1)

@@ -22,6 +22,8 @@ W_PASSES = N_SOURCE // (P * PACK)
 HALF = 256
 J_TILES = C // P
 RUN = 4
+RUNS = C // (2 * 2 * RUN)
+VECTOR_RUNS = (20, 24)
 
 FLOPS = 2 * B * C * N_TARGET * N_SOURCE + 2 * B * O * C * N_TARGET
 
@@ -34,10 +36,10 @@ def tile_stsgcm_pb_kernel(tc, h1, A_mid, W1, b1, out):
         psum_t = stack.enter_context(tc.psum_pool(name="psum_t", bufs=2))
         psum_g = stack.enter_context(tc.psum_pool(name="psum_g", bufs=2))
         psum_y = stack.enter_context(tc.psum_pool(name="psum_y", bufs=4))
+        stack.enter_context(tc.manual_schedule())
 
         bias_rows = keep.tile([P, P], BF16, name="bias_rows")
         nc.vector.memset(bias_rows[:], 0.0)
-        nc.sync.dma_start(out=bias_rows[0 : O // P, :], in_=b1.rearrange("(t p) -> t p", p=P))
         ident_f32 = keep.tile([P, P], F32, name="ident_f32")
         nc.vector.memset(ident_f32[:], 0.0)
         make_identity(nc, ident_f32[:], nomemset=True)
@@ -52,31 +54,38 @@ def tile_stsgcm_pb_kernel(tc, h1, A_mid, W1, b1, out):
         h_raw = [[keep.tile([P, PACK, C], BF16, name="h_raw%d_%d" % (b, s)) for s in range(W_PASSES)] for b in range(B)]
         w_raw = [keep.tile([P, 2, C], BF16, name="w_raw%d" % jt) for jt in range(J_TILES)]
 
-        def load_a(u):
+        def load_a(u, s):
+            cols = slice(P * PACK * s, P * PACK * (s + 1))
             nc.sync.dma_start(
-                out=a_raw[u][:], in_=A_mid[HALF * u : HALF * (u + 1), :].rearrange("(p e) w -> p e w", e=2)
+                out=a_raw[u][:, :, cols], in_=A_mid[HALF * u : HALF * (u + 1), cols].rearrange("(p e) w -> p e w", e=2)
             )
 
-        def load_h(b):
-            for s in range(W_PASSES):
-                for u in range(2):
-                    first = P * PACK * s + HALF * u
-                    nc.sync.dma_start(
-                        out=h_raw[b][s][:, 2 * u : 2 * u + 2, :],
-                        in_=h1[first : first + HALF, b, :].rearrange("(p e) c -> p e c", e=2),
-                    )
+        def load_h(b, s):
+            for u in range(2):
+                first = P * PACK * s + HALF * u
+                nc.sync.dma_start(
+                    out=h_raw[b][s][:, 2 * u : 2 * u + 2, :],
+                    in_=h1[first : first + HALF, b, :].rearrange("(p e) c -> p e c", e=2),
+                )
 
         def load_w(jt):
             nc.sync.dma_start(
                 out=w_raw[jt][:], in_=W1.rearrange("(v t p) c -> t p v c", v=2, p=P)[jt]
             )
 
-        load_h(0)
-        load_a(0)
-        load_a(1)
-        load_h(1)
+        load_h(0, 0)
+        load_a(0, 0)
+        load_a(0, 1)
+        load_h(0, 1)
+        load_a(0, 2)
+        load_h(0, 2)
+        for s in range(W_PASSES):
+            load_a(1, s)
+        for s in range(W_PASSES):
+            load_h(1, s)
         for jt in range(J_TILES):
             load_w(jt)
+        nc.sync.dma_start(out=bias_rows[0 : O // P, :], in_=b1.rearrange("(t p) -> t p", p=P))
 
         bias = keep.tile([P, O // P], F32, name="bias")
 
@@ -87,140 +96,245 @@ def tile_stsgcm_pb_kernel(tc, h1, A_mid, W1, b1, out):
 
         a_codes = [keep.tile([P, W_PASSES, HALF], U32, name="a_codes%d" % u, align_bytes=64) for u in range(2)]
         a_scales = [keep.tile([P, W_PASSES, HALF], U8, name="a_scales%d" % u, align_bytes=64) for u in range(2)]
+        a_grouped = [[keep.tile([P, HALF, PACK], BF16, name="a_grouped%d_%d" % (u, s), align_bytes=64) for s in range(W_PASSES)] for u in range(2)]
+        a_banks = {}
 
-        def prepare_a(u):
-            for s in range(W_PASSES):
-                a_ps = psum_t.tile([P, 2, HALF], F32, name="a_ps", tag="t")
-                for e in range(2):
-                    words = a_raw[u][:, e, :].bitcast(F32)
-                    for uw in range(2):
-                        first = HALF * s + P * uw
-                        nc.tensor.transpose(
-                            out=a_ps[:, uw, P * e : P * (e + 1)], in_=words[:, first : first + P], identity=ident_f32[:]
-                        )
-                a_grouped = keep.tile([P, HALF, PACK], BF16, name="a_grouped%d_%d" % (u, s), align_bytes=64)
-                nc.scalar.copy(out=a_grouped[:].bitcast(F32), in_=a_ps[:].rearrange("p u i -> p i u"))
-                nc.vector.quantize_mx(
-                    out=a_codes[u][:, s, :].bitcast(FP8X4),
-                    scales=a_scales[u][:, s, :],
-                    in_=a_grouped[:].rearrange("p i t -> p (i t)"),
-                )
+        def transpose_a(u, s):
+            a_ps = psum_y.tile([P, 2, HALF], F32, name="a_ps", tag="y")
+            for e in range(2):
+                words = a_raw[u][:, e, :].bitcast(F32)
+                for uw in range(2):
+                    first = HALF * s + P * uw
+                    nc.tensor.transpose(
+                        out=a_ps[:, uw, P * e : P * (e + 1)], in_=words[:, first : first + P], identity=ident_f32[:]
+                    )
+            a_banks[u, s] = a_ps
+
+        def copy_a(u, s):
+            nc.scalar.copy(out=a_grouped[u][s][:].bitcast(F32), in_=a_banks[u, s][:].rearrange("p u i -> p i u"))
+
+        def quantise_a(u, s):
+            nc.vector.quantize_mx(
+                out=a_codes[u][:, s, :].bitcast(FP8X4),
+                scales=a_scales[u][:, s, :],
+                in_=a_grouped[u][s][:].rearrange("p i t -> p (i t)"),
+            )
 
         h_codes = [[keep.tile([P, C], U32, name="h_codes%d_%d" % (b, s), align_bytes=64) for s in range(W_PASSES)] for b in range(B)]
         h_scales = [[keep.tile([P, C], U8, name="h_scales%d_%d" % (b, s), align_bytes=64) for s in range(W_PASSES)] for b in range(B)]
+        h_grouped = [[keep.tile([P, C, PACK], BF16, name="h_grouped%d_%d" % (b, s), align_bytes=64) for s in range(W_PASSES)] for b in range(B)]
 
-        def prepare_h(b):
-            for s in range(W_PASSES):
-                h_grouped = keep.tile([P, C, PACK], BF16, name="h_grouped%d_%d" % (b, s), align_bytes=64)
-                src = h_raw[b][s][:].rearrange("p t (u q i e) -> p u e q t i", u=2, i=RUN, e=2)
-                dst = h_grouped[:].rearrange("p (u e q i) t -> p u e q t i", u=2, e=2, i=RUN)
-                for e in range(2):
-                    nc.vector.tensor_copy(out=dst[:, 0, e], in_=src[:, 0, e])
-                    nc.scalar.copy(out=dst[:, 1, e], in_=src[:, 1, e])
-                nc.vector.quantize_mx(
-                    out=h_codes[b][s][:].bitcast(FP8X4),
-                    scales=h_scales[b][s][:],
-                    in_=h_grouped[:].rearrange("p c t -> p (c t)"),
-                )
+        def regroup(copy, b, s, runs):
+            src = h_raw[b][s][:].rearrange("p t (u q i e) -> p u e q t i", u=2, i=RUN, e=2)
+            dst = h_grouped[b][s][:].rearrange("p (u e q i) t -> p u e q t i", u=2, e=2, i=RUN)
+            for e in range(2):
+                copy(out=dst[:, :, e, runs], in_=src[:, :, e, runs])
+
+        def regroup_v(b, s):
+            regroup(nc.vector.tensor_copy, b, s, slice(0, VECTOR_RUNS[b]))
+
+        def regroup_s(b, s):
+            regroup(nc.scalar.copy, b, s, slice(VECTOR_RUNS[b], RUNS))
+
+        def quantise_h(b, s):
+            nc.vector.quantize_mx(
+                out=h_codes[b][s][:].bitcast(FP8X4),
+                scales=h_scales[b][s][:],
+                in_=h_grouped[b][s][:].rearrange("p c t -> p (c t)"),
+            )
 
         w_codes = [keep.tile([P, 2 * P], U32, name="w_codes%d" % jt, align_bytes=64) for jt in range(J_TILES)]
         w_scales = [keep.tile([P, 2 * P], U8, name="w_scales%d" % jt, align_bytes=64) for jt in range(J_TILES)]
+        w_grouped = [keep.tile([P, 2 * P, PACK], BF16, name="w_grouped%d" % jt, align_bytes=64) for jt in range(J_TILES)]
+        w_banks = {}
 
-        def prepare_w(jt):
-            w_ps = psum_t.tile([P, 2, 2 * P], F32, name="w_ps", tag="t")
+        def transpose_w(jt):
+            w_ps = psum_y.tile([P, 2, 2 * P], F32, name="w_ps", tag="y")
             for v in range(2):
                 words = w_raw[jt][:, v, :].bitcast(F32)
                 for uc in range(2):
                     nc.tensor.transpose(
                         out=w_ps[:, uc, P * v : P * (v + 1)], in_=words[:, P * uc : P * (uc + 1)], identity=ident_f32[:]
                     )
-            w_grouped = keep.tile([P, 2 * P, PACK], BF16, name="w_grouped%d" % jt, align_bytes=64)
-            nc.scalar.copy(out=w_grouped[:].bitcast(F32), in_=w_ps[:].rearrange("p u o -> p o u"))
+            w_banks[jt] = w_ps
+
+        def copy_w(jt):
+            nc.scalar.copy(out=w_grouped[jt][:].bitcast(F32), in_=w_banks[jt][:].rearrange("p u o -> p o u"))
+
+        def quantise_w(jt):
             nc.vector.quantize_mx(
                 out=w_codes[jt][:].bitcast(FP8X4),
                 scales=w_scales[jt][:],
-                in_=w_grouped[:].rearrange("p o t -> p (o t)"),
+                in_=w_grouped[jt][:].rearrange("p o t -> p (o t)"),
             )
 
         g_codes = [[keep.tile([P, HALF], U32, name="g_codes%d_%d" % (b, u), align_bytes=64) for u in range(2)] for b in range(B)]
         g_scales = [[keep.tile([P, HALF], U8, name="g_scales%d_%d" % (b, u), align_bytes=64) for u in range(2)] for b in range(B)]
+        g_grouped = [[keep.tile([P, HALF, PACK], BF16, name="g_grouped%d_%d" % (b, u), align_bytes=64) for u in range(2)] for b in range(B)]
+        g_banks = {}
 
-        def first_matmul(b, u):
-            g_grouped = keep.tile([P, HALF, PACK], BF16, name="g_grouped%d_%d" % (b, u), align_bytes=64)
-            for e in range(2):
-                g_ps = psum_g.tile([P, PACK, P], F32, name="g_ps")
-                for t in range(PACK):
-                    for s in range(W_PASSES):
-                        nc.tensor.matmul_mx(
-                            out=g_ps[:, t, :],
-                            lhsT=h_codes[b][s][:, P * t : P * (t + 1)].bitcast(FP8X4),
-                            lhsT_scale=h_scales[b][s][:, P * t : P * (t + 1)],
-                            rhs=a_codes[u][:, s, P * e : P * (e + 1)].bitcast(FP8X4),
-                            rhs_scale=a_scales[u][:, s, P * e : P * (e + 1)],
-                            start=(s == 0),
-                            stop=(s == W_PASSES - 1),
-                        )
-                nc.scalar.copy(out=g_grouped[:, P * e : P * (e + 1), :], in_=g_ps[:].rearrange("p t i -> p i t"))
+        def first_matmul(b, k):
+            u, e = divmod(k, 2)
+            g_ps = psum_g.tile([P, PACK, P], F32, name="g_ps")
+            for t in range(PACK):
+                for s in range(W_PASSES):
+                    nc.tensor.matmul_mx(
+                        out=g_ps[:, t, :],
+                        lhsT=h_codes[b][s][:, P * t : P * (t + 1)].bitcast(FP8X4),
+                        lhsT_scale=h_scales[b][s][:, P * t : P * (t + 1)],
+                        rhs=a_codes[u][:, s, P * e : P * (e + 1)].bitcast(FP8X4),
+                        rhs_scale=a_scales[u][:, s, P * e : P * (e + 1)],
+                        start=(s == 0),
+                        stop=(s == W_PASSES - 1),
+                    )
+            g_banks[b, k] = g_ps
+
+        def copy_g(b, k):
+            u, e = divmod(k, 2)
+            nc.scalar.copy(out=g_grouped[b][u][:, P * e : P * (e + 1), :], in_=g_banks[b, k][:].rearrange("p t i -> p i t"))
+
+        def quantise_g(b, u):
             nc.vector.quantize_mx(
                 out=g_codes[b][u][:].bitcast(FP8X4),
                 scales=g_scales[b][u][:],
-                in_=g_grouped[:].rearrange("p i t -> p (i t)"),
+                in_=g_grouped[b][u][:].rearrange("p i t -> p (i t)"),
             )
 
         out_sb = [keep.tile([P, PACK, C], F32, name="out_sb%d" % b) for b in range(B)]
+        y_banks = {}
+        gate_tiles = {}
+        h2_tiles = {}
+        o_banks = {}
 
-        def second_matmul(b, u):
-            for jp in range(J_TILES // 2):
-                o_ps = psum_t.tile([P, 2, 2 * P], F32, name="o_ps", tag="t")
-                for jl in range(2):
-                    jt = 2 * jp + jl
-                    y_ps = psum_y.tile([P, 2, HALF], F32, name="y_ps")
-                    for v in range(2):
-                        nc.tensor.matmul_mx(
-                            out=y_ps[:, v, :],
-                            lhsT=w_codes[jt][:, P * v : P * (v + 1)].bitcast(FP8X4),
-                            lhsT_scale=w_scales[jt][:, P * v : P * (v + 1)],
-                            rhs=g_codes[b][u][:].bitcast(FP8X4),
-                            rhs_scale=g_scales[b][u][:],
-                            start=True,
-                            stop=True,
-                        )
-                    gate = work.tile([P, HALF], F32, name="gate")
-                    nc.scalar.activation(
-                        out=gate[:], in_=y_ps[:, 1, :], func=ACT.Sigmoid, bias=bias[:, J_TILES + jt : J_TILES + jt + 1], scale=1.0
+        def second_matmul(b, u, jp):
+            for jt in (2 * jp, 2 * jp + 1):
+                y_ps = psum_y.tile([P, 2, HALF], F32, name="y_ps", tag="y")
+                for v in range(2):
+                    nc.tensor.matmul_mx(
+                        out=y_ps[:, v, :],
+                        lhsT=w_codes[jt][:, P * v : P * (v + 1)].bitcast(FP8X4),
+                        lhsT_scale=w_scales[jt][:, P * v : P * (v + 1)],
+                        rhs=g_codes[b][u][:].bitcast(FP8X4),
+                        rhs_scale=g_scales[b][u][:],
+                        start=True,
+                        stop=True,
                     )
-                    h2 = work.tile([P, HALF], F32, name="h2")
-                    nc.vector.scalar_tensor_tensor(
-                        out=h2[:], in0=y_ps[:, 0, :], scalar=bias[:, jt : jt + 1], in1=gate[:], op0=ALU.add, op1=ALU.mult
-                    )
-                    for e in range(2):
-                        nc.tensor.transpose(
-                            out=o_ps[:, e, P * jl : P * (jl + 1)], in_=h2[:, P * e : P * (e + 1)], identity=ident_f32[:]
-                        )
-                cols = slice(2 * P * jp, 2 * P * (jp + 1))
-                nc.vector.tensor_tensor(
-                    out=out_sb[b][:, 2 * u : 2 * u + 2, cols],
-                    in0=o_ps[:],
-                    in1=h_raw[b][1][:, 2 * u : 2 * u + 2, cols],
-                    op=ALU.max,
-                )
-                nc.sync.dma_start(
-                    out=out[HALF * u : HALF * (u + 1), b, cols].rearrange("(p e) j -> p e j", e=2),
-                    in_=out_sb[b][:, 2 * u : 2 * u + 2, cols],
-                )
+                y_banks[b, u, jt] = y_ps
 
-        prepare_h(0)
-        prepare_a(0)
-        prepare_a(1)
+        def gate(b, u, jp):
+            for jt in (2 * jp, 2 * jp + 1):
+                gate_sb = work.tile([P, HALF], F32, name="gate_sb")
+                nc.scalar.activation(
+                    out=gate_sb[:],
+                    in_=y_banks[b, u, jt][:, 1, :],
+                    func=ACT.Sigmoid,
+                    bias=bias[:, J_TILES + jt : J_TILES + jt + 1],
+                    scale=1.0,
+                )
+                gate_tiles[b, u, jt] = gate_sb
+
+        def product(b, u, jp):
+            for jt in (2 * jp, 2 * jp + 1):
+                h2 = work.tile([P, HALF], F32, name="h2")
+                nc.vector.scalar_tensor_tensor(
+                    out=h2[:],
+                    in0=y_banks[b, u, jt][:, 0, :],
+                    scalar=bias[:, jt : jt + 1],
+                    in1=gate_tiles[b, u, jt][:],
+                    op0=ALU.add,
+                    op1=ALU.mult,
+                )
+                h2_tiles[b, u, jt] = h2
+
+        def transpose_back(b, u, jp):
+            o_ps = psum_t.tile([P, 2, 2 * P], F32, name="o_ps", tag="t")
+            for jl in range(2):
+                for e in range(2):
+                    nc.tensor.transpose(
+                        out=o_ps[:, e, P * jl : P * (jl + 1)],
+                        in_=h2_tiles[b, u, 2 * jp + jl][:, P * e : P * (e + 1)],
+                        identity=ident_f32[:],
+                    )
+            o_banks[b, u, jp] = o_ps
+
+        def max_store(b, u, jp):
+            cols = slice(2 * P * jp, 2 * P * (jp + 1))
+            nc.vector.tensor_tensor(
+                out=out_sb[b][:, 2 * u : 2 * u + 2, cols],
+                in0=o_banks[b, u, jp][:],
+                in1=h_raw[b][1][:, 2 * u : 2 * u + 2, cols],
+                op=ALU.max,
+            )
+            nc.sync.dma_start(
+                out=out[HALF * u : HALF * (u + 1), b, cols].rearrange("(p e) j -> p e j", e=2),
+                in_=out_sb[b][:, 2 * u : 2 * u + 2, cols],
+            )
+
+        regroup_v(0, 0)
+        regroup_s(0, 0)
+        quantise_h(0, 0)
+        transpose_a(0, 0)
+        transpose_a(0, 1)
+        copy_a(0, 0)
+        copy_a(0, 1)
+        quantise_a(0, 0)
+        regroup_v(0, 1)
+        regroup_s(0, 1)
+        quantise_a(0, 1)
+        quantise_h(0, 1)
+        transpose_a(0, 2)
+        copy_a(0, 2)
+        regroup_v(0, 2)
+        regroup_s(0, 2)
+        quantise_a(0, 2)
+        quantise_h(0, 2)
+        for s in range(W_PASSES):
+            transpose_a(1, s)
+            copy_a(1, s)
+        quantise_a(1, 0)
+        regroup_v(1, 0)
+        quantise_a(1, 1)
+        quantise_a(1, 2)
+        regroup_s(1, 0)
+        quantise_h(1, 0)
         first_matmul(0, 0)
-        prepare_h(1)
-        prepare_bias()
-        for jt in range(J_TILES):
-            prepare_w(jt)
+        copy_g(0, 0)
         first_matmul(0, 1)
-        second_matmul(0, 0)
-        first_matmul(1, 0)
-        second_matmul(0, 1)
-        first_matmul(1, 1)
-        second_matmul(1, 0)
-        second_matmul(1, 1)
+        regroup_v(1, 1)
+        regroup_s(1, 1)
+        copy_g(0, 1)
+        regroup_v(1, 2)
+        regroup_s(1, 2)
+        quantise_h(1, 1)
+        quantise_g(0, 0)
+        quantise_h(1, 2)
+        first_matmul(0, 2)
+        first_matmul(0, 3)
+        copy_g(0, 2)
+        copy_g(0, 3)
+        for jt in range(J_TILES):
+            transpose_w(jt)
+            copy_w(jt)
+        quantise_w(0)
+        prepare_bias()
+        quantise_g(0, 1)
+        for jt in range(1, J_TILES):
+            quantise_w(jt)
+        units = [(b, u, jp) for b in range(B) for u in range(2) for jp in range(J_TILES // 2)]
+        for i in range(len(units) + 1):
+            if i < PACK:
+                first_matmul(1, i)
+            if i < len(units):
+                second_matmul(*units[i])
+            if i > 0:
+                transpose_back(*units[i - 1])
+            if i < len(units):
+                gate(*units[i])
+            if i < PACK:
+                copy_g(1, i)
+            if i < len(units):
+                product(*units[i])
+            if i > 0:
+                max_store(*units[i - 1])
+            if i in (1, 3):
+                quantise_g(1, i // 2)

@@ -50,14 +50,14 @@ def tile_stsgcm_pb_kernel(tc, h1, A_mid, W1, b1, out):
         nc.vector.memset(warm_in[:], 0.0)
         nc.scalar.activation(out=warm_out[:], in_=warm_in[:], func=ACT.Sigmoid)
 
-        a_raw = [keep.tile([P, 2, N_SOURCE], BF16, name="a_raw%d" % u) for u in range(2)]
+        a_raw = [[keep.tile([P, 2, P * PACK], BF16, name="a_raw%d_%d" % (u, s)) for s in range(W_PASSES)] for u in range(2)]
         h_raw = [[keep.tile([P, PACK, C], BF16, name="h_raw%d_%d" % (b, s)) for s in range(W_PASSES)] for b in range(B)]
         w_raw = [keep.tile([P, 2, C], BF16, name="w_raw%d" % jt) for jt in range(J_TILES)]
 
         def load_a(u, s):
             cols = slice(P * PACK * s, P * PACK * (s + 1))
             nc.sync.dma_start(
-                out=a_raw[u][:, :, cols], in_=A_mid[HALF * u : HALF * (u + 1), cols].rearrange("(p e) w -> p e w", e=2)
+                out=a_raw[u][s][:], in_=A_mid[HALF * u : HALF * (u + 1), cols].rearrange("(p e) w -> p e w", e=2)
             )
 
         def load_h(b, s):
@@ -102,11 +102,10 @@ def tile_stsgcm_pb_kernel(tc, h1, A_mid, W1, b1, out):
         def transpose_a(u, s):
             a_ps = psum_y.tile([P, 2, HALF], F32, name="a_ps", tag="y")
             for e in range(2):
-                words = a_raw[u][:, e, :].bitcast(F32)
+                words = a_raw[u][s][:, e, :].bitcast(F32)
                 for uw in range(2):
-                    first = HALF * s + P * uw
                     nc.tensor.transpose(
-                        out=a_ps[:, uw, P * e : P * (e + 1)], in_=words[:, first : first + P], identity=ident_f32[:]
+                        out=a_ps[:, uw, P * e : P * (e + 1)], in_=words[:, P * uw : P * (uw + 1)], identity=ident_f32[:]
                     )
             a_banks[u, s] = a_ps
 

@@ -22,8 +22,8 @@ W_PASSES = N_SOURCE // (P * PACK)
 HALF = 256
 J_TILES = C // P
 RUN = 4
-RUNS = C // (2 * 2 * RUN)
-VECTOR_RUNS = (20, 24)
+RUNS = C // (2 * RUN)
+VECTOR_RUNS = (16, 32)
 
 FLOPS = 2 * B * C * N_TARGET * N_SOURCE + 2 * B * O * C * N_TARGET
 
@@ -123,17 +123,17 @@ def tile_stsgcm_pb_kernel(tc, h1, A_mid, W1, b1, out):
         h_scales = [[keep.tile([P, C], U8, name="h_scales%d_%d" % (b, s), align_bytes=64) for s in range(W_PASSES)] for b in range(B)]
         h_grouped = [[keep.tile([P, C, PACK], BF16, name="h_grouped%d_%d" % (b, s), align_bytes=64) for s in range(W_PASSES)] for b in range(B)]
 
-        def regroup(copy, b, s, runs):
-            src = h_raw[b][s][:].rearrange("p t (u q i e) -> p u e q t i", u=2, i=RUN, e=2)
-            dst = h_grouped[b][s][:].rearrange("p (u e q i) t -> p u e q t i", u=2, e=2, i=RUN)
-            for e in range(2):
-                copy(out=dst[:, :, e, runs], in_=src[:, :, e, runs])
+        def regroup(copy, b, s, u, runs):
+            src = h_raw[b][s][:].rearrange("p t (u q i e) -> p u q t i e", u=2, i=RUN // 2, e=2)
+            dst = h_grouped[b][s][:].rearrange("p (u e q i) t -> p u q t i e", u=2, e=2, i=RUN // 2)
+            copy(out=dst[:, u, runs], in_=src[:, u, runs])
 
         def regroup_v(b, s):
-            regroup(nc.vector.tensor_copy, b, s, slice(0, VECTOR_RUNS[b]))
+            regroup(nc.vector.tensor_copy, b, s, 0, slice(0, RUNS))
+            regroup(nc.vector.tensor_copy, b, s, 1, slice(0, VECTOR_RUNS[b]))
 
         def regroup_s(b, s):
-            regroup(nc.scalar.copy, b, s, slice(VECTOR_RUNS[b], RUNS))
+            regroup(nc.scalar.copy, b, s, 1, slice(VECTOR_RUNS[b], RUNS))
 
         def quantise_h(b, s):
             nc.vector.quantize_mx(

@@ -32,7 +32,7 @@ def tile_stsgcm_pb_kernel(tc, h1, A_mid, W1, b1, out):
     nc = tc.nc
     with ExitStack() as stack:
         keep = stack.enter_context(tc.tile_pool(name="keep", bufs=1))
-        work = stack.enter_context(tc.tile_pool(name="work", bufs=4))
+        work = stack.enter_context(tc.tile_pool(name="work", bufs=6))
         psum_t = stack.enter_context(tc.psum_pool(name="psum_t", bufs=2))
         psum_g = stack.enter_context(tc.psum_pool(name="psum_g", bufs=2))
         psum_y = stack.enter_context(tc.psum_pool(name="psum_y", bufs=4))
@@ -205,8 +205,8 @@ def tile_stsgcm_pb_kernel(tc, h1, A_mid, W1, b1, out):
         h2_tiles = {}
         o_banks = {}
 
-        def second_matmul(b, u, jp):
-            for jt in (2 * jp, 2 * jp + 1):
+        def second_matmul(b, u, jts):
+            for jt in jts:
                 y_ps = psum_y.tile([P, 2, HALF], F32, name="y_ps", tag="y")
                 for v in range(2):
                     nc.tensor.matmul_mx(
@@ -220,8 +220,8 @@ def tile_stsgcm_pb_kernel(tc, h1, A_mid, W1, b1, out):
                     )
                 y_banks[b, u, jt] = y_ps
 
-        def gate(b, u, jp):
-            for jt in (2 * jp, 2 * jp + 1):
+        def gate(b, u, jts):
+            for jt in jts:
                 gate_sb = work.tile([P, HALF], F32, name="gate_sb")
                 nc.scalar.activation(
                     out=gate_sb[:],
@@ -232,8 +232,8 @@ def tile_stsgcm_pb_kernel(tc, h1, A_mid, W1, b1, out):
                 )
                 gate_tiles[b, u, jt] = gate_sb
 
-        def product(b, u, jp):
-            for jt in (2 * jp, 2 * jp + 1):
+        def product(b, u, jts):
+            for jt in jts:
                 h2 = work.tile([P, HALF], F32, name="h2")
                 nc.vector.scalar_tensor_tensor(
                     out=h2[:],
@@ -245,22 +245,22 @@ def tile_stsgcm_pb_kernel(tc, h1, A_mid, W1, b1, out):
                 )
                 h2_tiles[b, u, jt] = h2
 
-        def transpose_back(b, u, jp):
-            o_ps = psum_t.tile([P, 2, 2 * P], F32, name="o_ps", tag="t")
-            for jl in range(2):
+        def transpose_back(b, u, jts, pool, tag):
+            o_ps = pool.tile([P, 2, P * len(jts)], F32, name="o_ps", tag=tag)
+            for jl, jt in enumerate(jts):
                 for e in range(2):
                     nc.tensor.transpose(
                         out=o_ps[:, e, P * jl : P * (jl + 1)],
-                        in_=h2_tiles[b, u, 2 * jp + jl][:, P * e : P * (e + 1)],
+                        in_=h2_tiles[b, u, jt][:, P * e : P * (e + 1)],
                         identity=ident_f32[:],
                     )
-            o_banks[b, u, jp] = o_ps
+            o_banks[b, u, jts] = o_ps
 
-        def max_store(b, u, jp):
-            cols = slice(2 * P * jp, 2 * P * (jp + 1))
+        def max_store(b, u, jts):
+            cols = slice(P * jts[0], P * (jts[-1] + 1))
             nc.vector.tensor_tensor(
                 out=out_sb[b][:, 2 * u : 2 * u + 2, cols],
-                in0=o_banks[b, u, jp][:],
+                in0=o_banks[b, u, jts][:],
                 in1=h_raw[b][1][:, 2 * u : 2 * u + 2, cols],
                 op=ALU.max,
             )
@@ -319,21 +319,32 @@ def tile_stsgcm_pb_kernel(tc, h1, A_mid, W1, b1, out):
         quantise_g(0, 1)
         for jt in range(1, J_TILES):
             quantise_w(jt)
-        units = [(b, u, jp) for b in range(B) for u in range(2) for jp in range(J_TILES // 2)]
-        for i in range(len(units) + 1):
-            if i < PACK:
-                first_matmul(1, i)
-            if i < len(units):
-                second_matmul(*units[i])
-            if i > 0:
-                transpose_back(*units[i - 1])
-            if i < len(units):
-                gate(*units[i])
-            if i < PACK:
-                copy_g(1, i)
-            if i < len(units):
-                product(*units[i])
-            if i > 0:
-                max_store(*units[i - 1])
-            if i in (1, 3):
-                quantise_g(1, i // 2)
+        steps = [(b, u, jts) for b in range(B) for u in range(2) for jts in ((0, 1), (2, 3))]
+        waiting = []
+        for i, step in enumerate(steps):
+            blocks = [k for k in range(PACK) if 3 * k // 2 == i]
+            for k in blocks:
+                if k % 2 == 0:
+                    first_matmul(1, k)
+            second_matmul(*step)
+            for k in blocks:
+                if k % 2 == 1:
+                    first_matmul(1, k)
+            ready = waiting if i % 2 == 1 else []
+            for done in ready:
+                transpose_back(*done, psum_t, "t")
+            gate(*step)
+            for k in blocks:
+                copy_g(1, k)
+            product(*step)
+            for done in ready:
+                max_store(*done)
+            waiting = [done for done in waiting if done not in ready] + [step]
+            for k in blocks:
+                if k % 2 == 1:
+                    quantise_g(1, k // 2)
+        b, u, jts = steps[-1]
+        for jt in jts:
+            transpose_back(b, u, (jt,), psum_y, "y")
+        for jt in jts:
+            max_store(b, u, (jt,))

@@ -79,13 +79,13 @@ def tile_stsgcm_pb_kernel(tc, h1, A_mid, W1, b1, out):
         load_h(0, 1)
         load_a(0, 2)
         load_h(0, 2)
+        nc.sync.dma_start(out=bias_rows[0 : O // P, :], in_=b1.rearrange("(t p) -> t p", p=P))
         for s in range(W_PASSES):
             load_a(1, s)
         for s in range(W_PASSES):
             load_h(1, s)
         for jt in range(J_TILES):
             load_w(jt)
-        nc.sync.dma_start(out=bias_rows[0 : O // P, :], in_=b1.rearrange("(t p) -> t p", p=P))
 
         bias = keep.tile([P, O // P], F32, name="bias")
 
@@ -234,15 +234,18 @@ def tile_stsgcm_pb_kernel(tc, h1, A_mid, W1, b1, out):
 
         def product(b, u, jts):
             for jt in jts:
+                y_ps = y_banks[b, u, jt]
                 h2 = work.tile([P, HALF], F32, name="h2")
-                nc.vector.scalar_tensor_tensor(
-                    out=h2[:],
-                    in0=y_banks[b, u, jt][:, 0, :],
-                    scalar=bias[:, jt : jt + 1],
-                    in1=gate_tiles[b, u, jt][:],
-                    op0=ALU.add,
-                    op1=ALU.mult,
-                )
+                if jt == J_TILES - 1 and (b, u) != (B - 1, 1):
+                    value = work.tile([P, HALF], F32, name="value")
+                    nc.scalar.activation(
+                        out=value[:], in_=y_ps[:, 0, :], func=ACT.Identity, bias=bias[:, jt : jt + 1], scale=1.0
+                    )
+                    nc.gpsimd.tensor_tensor(out=h2[:], in0=value[:], in1=gate_tiles[b, u, jt][:], op=ALU.mult)
+                else:
+                    nc.vector.scalar_tensor_tensor(
+                        out=h2[:], in0=y_ps[:, 0, :], scalar=bias[:, jt : jt + 1], in1=gate_tiles[b, u, jt][:], op0=ALU.add, op1=ALU.mult
+                    )
                 h2_tiles[b, u, jt] = h2
 
         def transpose_back(b, u, jts, pool, tag):
@@ -287,6 +290,7 @@ def tile_stsgcm_pb_kernel(tc, h1, A_mid, W1, b1, out):
         regroup_s(0, 2)
         quantise_a(0, 2)
         quantise_h(0, 2)
+        prepare_bias()
         for s in range(W_PASSES):
             transpose_a(1, s)
             copy_a(1, s)
@@ -305,8 +309,8 @@ def tile_stsgcm_pb_kernel(tc, h1, A_mid, W1, b1, out):
         regroup_v(1, 2)
         regroup_s(1, 2)
         quantise_h(1, 1)
-        quantise_g(0, 0)
         quantise_h(1, 2)
+        quantise_g(0, 0)
         first_matmul(0, 2)
         first_matmul(0, 3)
         copy_g(0, 2)
@@ -315,7 +319,6 @@ def tile_stsgcm_pb_kernel(tc, h1, A_mid, W1, b1, out):
             transpose_w(jt)
             copy_w(jt)
         quantise_w(0)
-        prepare_bias()
         quantise_g(0, 1)
         for jt in range(1, J_TILES):
             quantise_w(jt)
@@ -323,13 +326,13 @@ def tile_stsgcm_pb_kernel(tc, h1, A_mid, W1, b1, out):
         waiting = []
         for i, step in enumerate(steps):
             blocks = [k for k in range(PACK) if 3 * k // 2 == i]
+            in_front = i == 0 or i % 2 == 1
+            if not in_front:
+                second_matmul(*step)
             for k in blocks:
-                if k % 2 == 0:
-                    first_matmul(1, k)
-            second_matmul(*step)
-            for k in blocks:
-                if k % 2 == 1:
-                    first_matmul(1, k)
+                first_matmul(1, k)
+            if in_front:
+                second_matmul(*step)
             ready = waiting if i % 2 == 1 else []
             for done in ready:
                 transpose_back(*done, psum_t, "t")

from contextlib import ExitStack

import concourse.mybir as mybir
from concourse.masks import make_identity

F32 = mybir.dt.float32
BF16 = mybir.dt.bfloat16
U32 = mybir.dt.uint32
U8 = mybir.dt.uint8
FP8X4 = mybir.dt.float8_e4m3fn_x4
ACT = mybir.ActivationFunctionType
ALU = mybir.AluOpType

P = 128
PACK = 4
N_TARGET = 512
N_SOURCE = 1536
B = 2
C = 512
O = 2 * C
W_PASSES = N_SOURCE // (P * PACK)
HALF = 256
J_TILES = C // P
RUN = 4
RUNS = C // (2 * RUN)
VECTOR_RUNS = (16, 32)

FLOPS = 2 * B * C * N_TARGET * N_SOURCE + 2 * B * O * C * N_TARGET


def tile_stsgcm_pb_kernel(tc, h1, A_mid, W1, b1, out):
    nc = tc.nc
    with ExitStack() as stack:
        keep = stack.enter_context(tc.tile_pool(name="keep", bufs=1))
        work = stack.enter_context(tc.tile_pool(name="work", bufs=6))
        psum_t = stack.enter_context(tc.psum_pool(name="psum_t", bufs=2))
        psum_g = stack.enter_context(tc.psum_pool(name="psum_g", bufs=2))
        psum_y = stack.enter_context(tc.psum_pool(name="psum_y", bufs=4))
        stack.enter_context(tc.manual_schedule())

        bias_rows = keep.tile([P, P], BF16, name="bias_rows")
        nc.vector.memset(bias_rows[:], 0.0)
        ident_f32 = keep.tile([P, P], F32, name="ident_f32")
        nc.vector.memset(ident_f32[:], 0.0)
        make_identity(nc, ident_f32[:], nomemset=True)
        ident_bf16 = keep.tile([P, P], BF16, name="ident_bf16")
        nc.vector.tensor_copy(out=ident_bf16[:], in_=ident_f32[:])
        warm_in = keep.tile([P, 1], F32, name="warm_in")
        warm_out = keep.tile([P, 1], F32, name="warm_out")
        nc.vector.memset(warm_in[:], 0.0)
        nc.scalar.activation(out=warm_out[:], in_=warm_in[:], func=ACT.Sigmoid)

        a_raw = [[keep.tile([P, 2, P * PACK], BF16, name="a_raw%d_%d" % (u, s)) for s in range(W_PASSES)] for u in range(2)]
        h_raw = [[keep.tile([P, PACK, C], BF16, name="h_raw%d_%d" % (b, s)) for s in range(W_PASSES)] for b in range(B)]
        w_raw = [keep.tile([P, 2, C], BF16, name="w_raw%d" % jt) for jt in range(J_TILES)]

        def load_a(u, s):
            cols = slice(P * PACK * s, P * PACK * (s + 1))
            nc.sync.dma_start(
                out=a_raw[u][s][:], in_=A_mid[HALF * u : HALF * (u + 1), cols].rearrange("(p e) w -> p e w", e=2)
            )

        def load_h(b, s):
            for u in range(2):
                first = P * PACK * s + HALF * u
                nc.sync.dma_start(
                    out=h_raw[b][s][:, 2 * u : 2 * u + 2, :],
                    in_=h1[first : first + HALF, b, :].rearrange("(p e) c -> p e c", e=2),
                )

        def load_w(jt):
            nc.sync.dma_start(
                out=w_raw[jt][:], in_=W1.rearrange("(v t p) c -> t p v c", v=2, p=P)[jt]
            )

        load_h(0, 0)
        load_a(0, 0)
        load_a(0, 1)
        load_h(0, 1)
        load_a(0, 2)
        load_h(0, 2)
        nc.sync.dma_start(out=bias_rows[0 : O // P, :], in_=b1.rearrange("(t p) -> t p", p=P))
        for s in range(W_PASSES):
            load_a(1, s)
        for s in range(W_PASSES):
            load_h(1, s)
        for jt in range(J_TILES):
            load_w(jt)

        bias = keep.tile([P, O // P], F32, name="bias")

        def prepare_bias():
            bias_ps = psum_t.tile([P, P], BF16, name="bias_ps", tag="t")
            nc.tensor.transpose(out=bias_ps[:], in_=bias_rows[:], identity=ident_bf16[:])
            nc.vector.tensor_copy(out=bias[:], in_=bias_ps[:, 0 : O // P])

        a_codes = [keep.tile([P, W_PASSES, HALF], U32, name="a_codes%d" % u, align_bytes=64) for u in range(2)]
        a_scales = [keep.tile([P, W_PASSES, HALF], U8, name="a_scales%d" % u, align_bytes=64) for u in range(2)]
        a_grouped = [[keep.tile([P, HALF, PACK], BF16, name="a_grouped%d_%d" % (u, s), align_bytes=64) for s in range(W_PASSES)] for u in range(2)]
        a_banks = {}

        def transpose_a(u, s):
            a_ps = psum_y.tile([P, 2, HALF], F32, name="a_ps", tag="y")
            for e in range(2):
                words = a_raw[u][s][:, e, :].bitcast(F32)
                for uw in range(2):
                    nc.tensor.transpose(
                        out=a_ps[:, uw, P * e : P * (e + 1)], in_=words[:, P * uw : P * (uw + 1)], identity=ident_f32[:]
                    )
            a_banks[u, s] = a_ps

        def copy_a(u, s):
            nc.scalar.copy(out=a_grouped[u][s][:].bitcast(F32), in_=a_banks[u, s][:].rearrange("p u i -> p i u"))

        def quantise_a(u, s):
            nc.vector.quantize_mx(
                out=a_codes[u][:, s, :].bitcast(FP8X4),
                scales=a_scales[u][:, s, :],
                in_=a_grouped[u][s][:].rearrange("p i t -> p (i t)"),
            )

        h_codes = [[keep.tile([P, C], U32, name="h_codes%d_%d" % (b, s), align_bytes=64) for s in range(W_PASSES)] for b in range(B)]
        h_scales = [[keep.tile([P, C], U8, name="h_scales%d_%d" % (b, s), align_bytes=64) for s in range(W_PASSES)] for b in range(B)]
        h_grouped = [[keep.tile([P, C, PACK], BF16, name="h_grouped%d_%d" % (b, s), align_bytes=64) for s in range(W_PASSES)] for b in range(B)]

        def regroup(copy, b, s, u, runs):
            src = h_raw[b][s][:].rearrange("p t (u q i e) -> p u q t i e", u=2, i=RUN // 2, e=2)
            dst = h_grouped[b][s][:].rearrange("p (u e q i) t -> p u q t i e", u=2, e=2, i=RUN // 2)
            copy(out=dst[:, u, runs], in_=src[:, u, runs])

        def regroup_v(b, s):
            regroup(nc.vector.tensor_copy, b, s, 0, slice(0, RUNS))
            regroup(nc.vector.tensor_copy, b, s, 1, slice(0, VECTOR_RUNS[b]))

        def regroup_s(b, s):
            regroup(nc.scalar.copy, b, s, 1, slice(VECTOR_RUNS[b], RUNS))

        def quantise_h(b, s):
            nc.vector.quantize_mx(
                out=h_codes[b][s][:].bitcast(FP8X4),
                scales=h_scales[b][s][:],
                in_=h_grouped[b][s][:].rearrange("p c t -> p (c t)"),
            )

        w_codes = [keep.tile([P, 2 * P], U32, name="w_codes%d" % jt, align_bytes=64) for jt in range(J_TILES)]
        w_scales = [keep.tile([P, 2 * P], U8, name="w_scales%d" % jt, align_bytes=64) for jt in range(J_TILES)]
        w_grouped = [keep.tile([P, 2 * P, PACK], BF16, name="w_grouped%d" % jt, align_bytes=64) for jt in range(J_TILES)]
        w_banks = {}

        def transpose_w(jt):
            w_ps = psum_y.tile([P, 2, 2 * P], F32, name="w_ps", tag="y")
            for v in range(2):
                words = w_raw[jt][:, v, :].bitcast(F32)
                for uc in range(2):
                    nc.tensor.transpose(
                        out=w_ps[:, uc, P * v : P * (v + 1)], in_=words[:, P * uc : P * (uc + 1)], identity=ident_f32[:]
                    )
            w_banks[jt] = w_ps

        def copy_w(jt):
            nc.scalar.copy(out=w_grouped[jt][:].bitcast(F32), in_=w_banks[jt][:].rearrange("p u o -> p o u"))

        def quantise_w(jt):
            nc.vector.quantize_mx(
                out=w_codes[jt][:].bitcast(FP8X4),
                scales=w_scales[jt][:],
                in_=w_grouped[jt][:].rearrange("p o t -> p (o t)"),
            )

        g_codes = [[keep.tile([P, HALF], U32, name="g_codes%d_%d" % (b, u), align_bytes=64) for u in range(2)] for b in range(B)]
        g_scales = [[keep.tile([P, HALF], U8, name="g_scales%d_%d" % (b, u), align_bytes=64) for u in range(2)] for b in range(B)]
        g_grouped = [[keep.tile([P, HALF, PACK], BF16, name="g_grouped%d_%d" % (b, u), align_bytes=64) for u in range(2)] for b in range(B)]
        g_banks = {}

        def first_matmul(b, k):
            u, e = divmod(k, 2)
            g_ps = psum_g.tile([P, PACK, P], F32, name="g_ps")
            for t in range(PACK):
                for s in range(W_PASSES):
                    nc.tensor.matmul_mx(
                        out=g_ps[:, t, :],
                        lhsT=h_codes[b][s][:, P * t : P * (t + 1)].bitcast(FP8X4),
                        lhsT_scale=h_scales[b][s][:, P * t : P * (t + 1)],
                        rhs=a_codes[u][:, s, P * e : P * (e + 1)].bitcast(FP8X4),
                        rhs_scale=a_scales[u][:, s, P * e : P * (e + 1)],
                        start=(s == 0),
                        stop=(s == W_PASSES - 1),
                    )
            g_banks[b, k] = g_ps

        def copy_g(b, k):
            u, e = divmod(k, 2)
            nc.scalar.copy(out=g_grouped[b][u][:, P * e : P * (e + 1), :], in_=g_banks[b, k][:].rearrange("p t i -> p i t"))

        def quantise_g(b, u):
            nc.vector.quantize_mx(
                out=g_codes[b][u][:].bitcast(FP8X4),
                scales=g_scales[b][u][:],
                in_=g_grouped[b][u][:].rearrange("p i t -> p (i t)"),
            )

        out_sb = [keep.tile([P, PACK, C], F32, name="out_sb%d" % b) for b in range(B)]
        y_banks = {}
        gate_tiles = {}
        h2_tiles = {}
        o_banks = {}

        def second_matmul(b, u, jts):
            for jt in jts:
                y_ps = psum_y.tile([P, 2, HALF], F32, name="y_ps", tag="y")
                for v in range(2):
                    nc.tensor.matmul_mx(
                        out=y_ps[:, v, :],
                        lhsT=w_codes[jt][:, P * v : P * (v + 1)].bitcast(FP8X4),
                        lhsT_scale=w_scales[jt][:, P * v : P * (v + 1)],
                        rhs=g_codes[b][u][:].bitcast(FP8X4),
                        rhs_scale=g_scales[b][u][:],
                        start=True,
                        stop=True,
                    )
                y_banks[b, u, jt] = y_ps

        def gate(b, u, jts):
            for jt in jts:
                gate_sb = work.tile([P, HALF], F32, name="gate_sb")
                nc.scalar.activation(
                    out=gate_sb[:],
                    in_=y_banks[b, u, jt][:, 1, :],
                    func=ACT.Sigmoid,
                    bias=bias[:, J_TILES + jt : J_TILES + jt + 1],
                    scale=1.0,
                )
                gate_tiles[b, u, jt] = gate_sb

        def product(b, u, jts):
            for jt in jts:
                y_ps = y_banks[b, u, jt]
                h2 = work.tile([P, HALF], F32, name="h2")
                if jt == J_TILES - 1 and (b, u) != (B - 1, 1):
                    value = work.tile([P, HALF], F32, name="value")
                    nc.scalar.activation(
                        out=value[:], in_=y_ps[:, 0, :], func=ACT.Identity, bias=bias[:, jt : jt + 1], scale=1.0
                    )
                    nc.gpsimd.tensor_tensor(out=h2[:], in0=value[:], in1=gate_tiles[b, u, jt][:], op=ALU.mult)
                else:
                    nc.vector.scalar_tensor_tensor(
                        out=h2[:], in0=y_ps[:, 0, :], scalar=bias[:, jt : jt + 1], in1=gate_tiles[b, u, jt][:], op0=ALU.add, op1=ALU.mult
                    )
                h2_tiles[b, u, jt] = h2

        def transpose_back(b, u, jts, pool, tag):
            o_ps = pool.tile([P, 2, P * len(jts)], F32, name="o_ps", tag=tag)
            for jl, jt in enumerate(jts):
                for e in range(2):
                    nc.tensor.transpose(
                        out=o_ps[:, e, P * jl : P * (jl + 1)],
                        in_=h2_tiles[b, u, jt][:, P * e : P * (e + 1)],
                        identity=ident_f32[:],
                    )
            o_banks[b, u, jts] = o_ps

        def max_store(b, u, jts):
            cols = slice(P * jts[0], P * (jts[-1] + 1))
            nc.vector.tensor_tensor(
                out=out_sb[b][:, 2 * u : 2 * u + 2, cols],
                in0=o_banks[b, u, jts][:],
                in1=h_raw[b][1][:, 2 * u : 2 * u + 2, cols],
                op=ALU.max,
            )
            nc.sync.dma_start(
                out=out[HALF * u : HALF * (u + 1), b, cols].rearrange("(p e) j -> p e j", e=2),
                in_=out_sb[b][:, 2 * u : 2 * u + 2, cols],
            )

        regroup_v(0, 0)
        regroup_s(0, 0)
        quantise_h(0, 0)
        transpose_a(0, 0)
        transpose_a(0, 1)
        copy_a(0, 0)
        copy_a(0, 1)
        quantise_a(0, 0)
        regroup_v(0, 1)
        regroup_s(0, 1)
        quantise_a(0, 1)
        quantise_h(0, 1)
        transpose_a(0, 2)
        copy_a(0, 2)
        regroup_v(0, 2)
        regroup_s(0, 2)
        quantise_a(0, 2)
        quantise_h(0, 2)
        prepare_bias()
        for s in range(W_PASSES):
            transpose_a(1, s)
            copy_a(1, s)
        quantise_a(1, 0)
        regroup_v(1, 0)
        quantise_a(1, 1)
        quantise_a(1, 2)
        regroup_s(1, 0)
        quantise_h(1, 0)
        first_matmul(0, 0)
        copy_g(0, 0)
        first_matmul(0, 1)
        regroup_v(1, 1)
        regroup_s(1, 1)
        copy_g(0, 1)
        regroup_v(1, 2)
        regroup_s(1, 2)
        quantise_h(1, 1)
        quantise_h(1, 2)
        quantise_g(0, 0)
        first_matmul(0, 2)
        first_matmul(0, 3)
        copy_g(0, 2)
        copy_g(0, 3)
        for jt in range(J_TILES):
            transpose_w(jt)
            copy_w(jt)
        quantise_w(0)
        quantise_g(0, 1)
        for jt in range(1, J_TILES):
            quantise_w(jt)
        steps = [(b, u, jts) for b in range(B) for u in range(2) for jts in ((0, 1), (2, 3))]
        waiting = []
        for i, step in enumerate(steps):
            blocks = [k for k in range(PACK) if 3 * k // 2 == i]
            in_front = i == 0 or i % 2 == 1
            if not in_front:
                second_matmul(*step)
            for k in blocks:
                first_matmul(1, k)
            if in_front:
                second_matmul(*step)
            ready = waiting if i % 2 == 1 else []
            for done in ready:
                transpose_back(*done, psum_t, "t")
            gate(*step)
            for k in blocks:
                copy_g(1, k)
            product(*step)
            for done in ready:
                max_store(*done)
            waiting = [done for done in waiting if done not in ready] + [step]
            for k in blocks:
                if k % 2 == 1:
                    quantise_g(1, k // 2)
        b, u, jts = steps[-1]
        for jt in jts:
            transpose_back(b, u, (jt,), psum_y, "y")
        for jt in jts:
            max_store(b, u, (jt,))
